import numpy as np
import ml_dtypes


def mxq(x, axis, fmt="e4m3"):
    dtype, down = {"e4m3": (ml_dtypes.float8_e4m3fn, 7), "e5m2": (ml_dtypes.float8_e5m2, 14)}[fmt]
    v = np.moveaxis(np.asarray(x, np.float32).astype(ml_dtypes.bfloat16).astype(np.float64), axis, -1)
    blocks = v.reshape(v.shape[:-1] + (-1, 32))
    amax = np.abs(blocks).max(-1, keepdims=True)
    byte = np.maximum(np.where(amax > 0, np.frexp(amax)[1] - 1 + 127, 0) - down, 1)
    scale = np.exp2(byte - 127.0)
    codes = (blocks / scale).astype(np.float32).astype(dtype).astype(np.float64)
    return np.moveaxis((codes * scale).reshape(v.shape), -1, axis)


WIDE = False


def mx_kscale(k):
    if not WIDE:
        return np.ones(k)
    levels = np.array([10, -10, 5, -5, 0])
    if k % 512:
        return np.exp2(np.random.permutation(np.resize(levels, k // 32))).repeat(32)
    a = np.empty((k // 512, 16))
    for p in range(k // 512):
        a[p, :8] = np.random.permutation(np.resize(levels, 8))
        for g in range(8):
            far = levels[np.abs(levels - a[p, g]) >= 10]
            a[p, g + 8] = far[np.random.randint(len(far))]
    return np.exp2(a.ravel()).repeat(32)


BF16 = ml_dtypes.bfloat16


def bf(x):
    return np.asarray(x, np.float32).astype(BF16)


def f64(x):
    return np.asarray(x).astype(np.float64)


B, S, I, Q = 4096, 3, 512, 512
LN_EPS = 1e-5


def setup_inputs():
    s = mx_kscale(I)
    return {"language_features": bf(np.random.standard_normal((B, I)) * s),
            "W": bf(np.random.standard_normal((S, I, Q)) / np.sqrt(I) / s[None, :, None]),
            "b": bf(np.random.standard_normal((S, Q)) * 0.2),
            "amplitude_weights": bf(np.random.standard_normal((S, Q))),
            "phase_weights": bf(np.random.standard_normal((S, Q))),
            "ln_gamma": bf(1.0 + 0.1 * np.random.standard_normal(Q)),
            "ln_beta": bf(0.1 * np.random.standard_normal(Q))}


def reference(language_features, W, b, amplitude_weights, phase_weights, ln_gamma, ln_beta):
    xq = mxq(f64(language_features), 1, "e4m3")
    wq = mxq(f64(W), 1, "e4m3")
    states = (xq @ wq).transpose(1, 0, 2) + f64(b)[None, :, :]
    a = f64(amplitude_weights)
    e = np.exp(a - a.max(axis=0, keepdims=True))
    amplitudes = e / e.sum(axis=0, keepdims=True)
    mix = amplitudes * np.cos(f64(phase_weights))
    sup = states * mix[None, :, :]
    mean = sup.mean(axis=-1, keepdims=True)
    var = sup.var(axis=-1, keepdims=True)
    return (sup - mean) * (1.0 / np.sqrt(var + LN_EPS)) * f64(ln_gamma) + f64(ln_beta)

@@ -1,0 +1,356 @@
+from contextlib import ExitStack
+
+import concourse.mybir as mybir
+from concourse.masks import make_identity
+
+F32 = mybir.dt.float32
+BF16 = mybir.dt.bfloat16
+U32 = mybir.dt.uint32
+U8 = mybir.dt.uint8
+FP8X4 = mybir.dt.float8_e4m3fn_x4
+ALU = mybir.AluOpType
+ACT = mybir.ActivationFunctionType
+
+P = 128
+ROWS = 4096
+K = 512
+Q = 512
+STATES = 3
+LN_EPS = 1e-5
+
+PACK = 4
+ROW_TILES = ROWS // P
+GROUP_TILES = 4
+GROUP_ROWS = GROUP_TILES * P
+GROUPS = ROW_TILES // GROUP_TILES
+Q_SLICES = Q // P
+UNITS = GROUPS * STATES
+TILES = UNITS * GROUP_TILES
+LAG = GROUP_TILES - 1
+
+TWO_PI_HIGH = 6.28125
+TWO_PI_MID = 0.0019350051879882812
+TWO_PI_LOW = 3.019916050561733e-07
+ONE_OVER_TWO_PI = 0.15915494309189535
+ROUND_TO_WHOLE = 12582912.0
+
+FLOPS = 2 * ROWS * STATES * K * Q
+
+
+def tile_quantumsuperposition_t_kernel(
+    tc, language_features, W, b, amplitude_weights, phase_weights, ln_gamma, ln_beta, out
+):
+    nc = tc.nc
+    with ExitStack() as ctx:
+        consts = ctx.enter_context(tc.tile_pool(name="consts", bufs=1))
+        x_in = ctx.enter_context(tc.tile_pool(name="x_in", bufs=GROUPS))
+        x_mx = ctx.enter_context(tc.tile_pool(name="x_mx", bufs=2))
+        w_in = ctx.enter_context(tc.tile_pool(name="w_in", bufs=STATES))
+        sup_t_pool = ctx.enter_context(tc.tile_pool(name="sup_t", bufs=3))
+        y_pool = ctx.enter_context(tc.tile_pool(name="y", bufs=3 * GROUP_TILES))
+        stat_pool = ctx.enter_context(tc.tile_pool(name="stat", bufs=4))
+        psum_acc = ctx.enter_context(tc.psum_pool(name="psum_acc", bufs=3))
+        psum_sup = ctx.enter_context(tc.psum_pool(name="psum_sup", bufs=GROUP_TILES))
+        psum_x = ctx.enter_context(tc.psum_pool(name="psum_x", bufs=1))
+        ctx.enter_context(tc.manual_schedule())
+
+        x_view = language_features.rearrange("(p i) k -> p i k", i=ROW_TILES)
+        out_view = out.rearrange("(p i) s q -> p i s q", i=ROW_TILES)
+
+        vec_rows = consts.tile([P, P], BF16)
+        nc.vector.memset(vec_rows[:], 0.0)
+        vec_count = STATES * Q_SLICES
+        for n, vec in enumerate((b, amplitude_weights, phase_weights)):
+            nc.scalar.dma_start(
+                out=vec_rows[n * vec_count : (n + 1) * vec_count, :],
+                in_=vec.rearrange("s (j p) -> (s j) p", p=P),
+            )
+        gain_shift_row = consts.tile([P, 2, Q], BF16)
+        nc.vector.memset(gain_shift_row[:], 0.0)
+        nc.scalar.dma_start(out=gain_shift_row[0:1, 0, :], in_=ln_gamma.unsqueeze(0))
+        nc.scalar.dma_start(out=gain_shift_row[0:1, 1, :], in_=ln_beta.unsqueeze(0))
+
+        w_rows = {}
+        x_rows = {}
+
+        def load_w(s):
+            rows = w_in.tile([P, PACK * Q], BF16, name="w_rows")
+            nc.sync.dma_start(
+                out=rows[:], in_=W[s, :, :].rearrange("(p t) q -> p (t q)", t=PACK)
+            )
+            w_rows[s] = rows
+
+        def load_x(g):
+            rows = x_in.tile([P, GROUP_TILES * K], BF16, name="x_rows")
+            nc.sync.dma_start(
+                out=rows[:].rearrange("p (i k) -> p i k", i=GROUP_TILES),
+                in_=x_view[:, g * GROUP_TILES : (g + 1) * GROUP_TILES, :],
+            )
+            x_rows[g] = rows
+
+        load_x(0)
+        for s in range(STATES):
+            load_w(s)
+        for g in range(1, GROUPS):
+            load_x(g)
+
+        ident = consts.tile([P, P], F32)
+        make_identity(nc, ident[:])
+        ones = consts.tile([P, P], BF16)
+        nc.vector.memset(ones[:], 1.0)
+        eps = consts.tile([P, 1], F32)
+        nc.vector.memset(eps[:], LN_EPS)
+
+        w_codes = consts.tile([P, STATES * Q], U32, align_bytes=64)
+        w_scales = consts.tile([P, STATES * Q], U8, align_bytes=64)
+
+        def quantise_w(s):
+            grouped = w_in.tile([P, Q * PACK], BF16, name="w_grouped", align_bytes=64)
+            nc.vector.tensor_copy(
+                out=grouped[:].rearrange("p (q t) -> p q t", t=PACK),
+                in_=w_rows[s][:].rearrange("p (t q) -> p q t", t=PACK),
+            )
+            nc.vector.quantize_mx(
+                out=w_codes[:, s * Q : (s + 1) * Q].bitcast(FP8X4),
+                scales=w_scales[:, s * Q : (s + 1) * Q],
+                in_=grouped[:],
+            )
+
+        x_t = {}
+        x_grouped = {}
+        x_codes = {}
+        x_scales = {}
+
+        def x_transposes(g, pair):
+            words = x_rows[g][:].bitcast(F32)
+            x_t_pair = psum_x.tile([P, 2, 2 * P], F32, tag="small")
+            for ii in range(2):
+                for u in range(2):
+                    first = (2 * pair + ii) * 2 * P
+                    nc.tensor.transpose(
+                        x_t_pair[:, u, ii * P : (ii + 1) * P],
+                        words[:, first + u : first + 2 * P : 2],
+                        ident[:],
+                    )
+            x_t[g, pair] = x_t_pair
+
+        def x_regroup(g, pair):
+            if pair == 0:
+                grouped = x_mx.tile([P, GROUP_ROWS * PACK], BF16, name="x_grouped", align_bytes=64)
+                x_grouped[g] = grouped
+            grouped_words = x_grouped[g][:].bitcast(F32).rearrange("p (c u) -> p c u", u=2)
+            nc.scalar.copy(
+                out=grouped_words[:, pair * 2 * P : (pair + 1) * 2 * P, :],
+                in_=x_t[g, pair][:].rearrange("p u c -> p c u"),
+            )
+
+        def x_quantise(g):
+            codes = x_mx.tile([P, GROUP_ROWS], U32, name="x_codes", align_bytes=64)
+            scales = x_mx.tile([P, GROUP_ROWS], U8, name="x_scales", align_bytes=64)
+            nc.vector.quantize_mx(
+                out=codes[:].bitcast(FP8X4), scales=scales[:], in_=x_grouped[g][:]
+            )
+            x_codes[g] = codes
+            x_scales[g] = scales
+
+        vec_rows_f32 = consts.tile([P, P], F32)
+        nc.vector.tensor_copy(out=vec_rows_f32[:], in_=vec_rows[:])
+        vec_t = psum_x.tile([P, P], F32, tag="small")
+        nc.tensor.transpose(vec_t[:], vec_rows_f32[:], ident[:])
+        vecs = consts.tile([P, 3, STATES, Q_SLICES], F32)
+        nc.vector.tensor_copy(
+            out=vecs[:].rearrange("p n s j -> p (n s j)"), in_=vec_t[:, 0 : 3 * vec_count]
+        )
+        bias = vecs[:, 0, :, :]
+        amplitude = vecs[:, 1, :, :]
+        phase = vecs[:, 2, :, :]
+        per_state = [P, STATES, Q_SLICES]
+
+        top = consts.tile([P, Q_SLICES], F32)
+        nc.vector.tensor_max(out=top[:], in0=amplitude[:, 0, :], in1=amplitude[:, 1, :])
+        nc.vector.tensor_max(out=top[:], in0=top[:], in1=amplitude[:, 2, :])
+        shifted = consts.tile(per_state, F32)
+        nc.vector.tensor_tensor(
+            out=shifted[:], in0=amplitude, in1=top[:].unsqueeze(1).to_broadcast(per_state),
+            op=ALU.subtract,
+        )
+        expd = consts.tile(per_state, F32)
+        nc.scalar.activation(out=expd[:], in_=shifted[:], func=ACT.Exp)
+
+        turns = consts.tile(per_state, F32)
+        nc.vector.tensor_scalar(
+            out=turns[:], in0=phase, scalar1=ONE_OVER_TWO_PI, scalar2=ROUND_TO_WHOLE,
+            op0=ALU.mult, op1=ALU.add,
+        )
+        nc.vector.tensor_scalar_sub(out=turns[:], in0=turns[:], scalar1=ROUND_TO_WHOLE)
+        rest_a = consts.tile(per_state, F32)
+        nc.vector.scalar_tensor_tensor(
+            out=rest_a[:], in0=turns[:], scalar=-TWO_PI_HIGH, in1=phase, op0=ALU.mult, op1=ALU.add
+        )
+        rest_b = consts.tile(per_state, F32)
+        nc.vector.scalar_tensor_tensor(
+            out=rest_b[:], in0=turns[:], scalar=-TWO_PI_MID, in1=rest_a[:], op0=ALU.mult, op1=ALU.add
+        )
+        rest = consts.tile(per_state, F32)
+        nc.vector.scalar_tensor_tensor(
+            out=rest[:], in0=turns[:], scalar=-TWO_PI_LOW, in1=rest_b[:], op0=ALU.mult, op1=ALU.add
+        )
+        half_sin = consts.tile(per_state, F32)
+        nc.scalar.activation(out=half_sin[:], in_=rest[:], func=ACT.Sin, scale=0.5)
+
+        gain_shift = consts.tile([P, 2, Q], F32)
+        for n in range(2):
+            spread = psum_acc.tile([P, Q], F32, name="acc")
+            nc.tensor.matmul(
+                out=spread[:], lhsT=ones[:], rhs=gain_shift_row[:, n, :], start=True, stop=True
+            )
+            nc.vector.tensor_copy(out=gain_shift[:, n, :], in_=spread[:])
+        gain = gain_shift[:, 0, :]
+        shift = gain_shift[:, 1, :]
+
+        for pair in range(2):
+            x_transposes(0, pair)
+            x_regroup(0, pair)
+        quantise_w(0)
+
+        total = consts.tile([P, Q_SLICES], F32)
+        nc.vector.tensor_add(out=total[:], in0=expd[:, 0, :], in1=expd[:, 1, :])
+        nc.vector.tensor_add(out=total[:], in0=total[:], in1=expd[:, 2, :])
+        one_over_total = consts.tile([P, Q_SLICES], F32)
+        nc.vector.reciprocal(out=one_over_total[:], in_=total[:])
+        cosine = consts.tile(per_state, F32)
+        nc.vector.tensor_mul(out=cosine[:], in0=half_sin[:], in1=half_sin[:])
+        nc.vector.tensor_scalar(
+            out=cosine[:], in0=cosine[:], scalar1=-2.0, scalar2=1.0, op0=ALU.mult, op1=ALU.add
+        )
+        mix = consts.tile(per_state, F32)
+        nc.vector.tensor_mul(out=mix[:], in0=expd[:], in1=cosine[:])
+        nc.vector.tensor_mul(
+            out=mix[:], in0=mix[:], in1=one_over_total[:].unsqueeze(1).to_broadcast(per_state)
+        )
+        bias_mix = consts.tile(per_state, F32)
+        nc.vector.tensor_mul(out=bias_mix[:], in0=bias, in1=mix[:])
+
+        x_quantise(0)
+        quantise_w(1)
+        quantise_w(2)
+
+        table_warmer = consts.tile([P, 1], F32)
+        nc.scalar.activation(
+            out=table_warmer[:], in_=eps[:], func=ACT.Abs_reciprocal_sqrt, bias=eps[:, 0:1], scale=1.0
+        )
+
+        acc = {}
+        sup_t = {}
+        sup = {}
+        halves = {}
+        mean_var = {}
+        rstd = {}
+        y = {}
+
+        def slice_products(u, j):
+            g, s = divmod(u, STATES)
+            cols = slice(s * Q + j * P, s * Q + (j + 1) * P)
+            acc_j = psum_acc.tile([P, GROUP_ROWS], F32, name="acc")
+            nc.tensor.matmul_mx(
+                out=acc_j[:],
+                lhsT=w_codes[:, cols].bitcast(FP8X4),
+                lhsT_scale=w_scales[:, cols],
+                rhs=x_codes[g][:].bitcast(FP8X4),
+                rhs_scale=x_scales[g][:],
+                start=True,
+                stop=True,
+            )
+            acc[u, j] = acc_j
+
+        def slice_mix(u, j):
+            s = u % STATES
+            if j == 0:
+                sup_t_u = sup_t_pool.tile([P, Q_SLICES, GROUP_ROWS], F32, name="sup_t")
+                sup_t[u] = sup_t_u
+            nc.scalar.activation(
+                out=sup_t[u][:, j, :], in_=acc[u, j][:], func=ACT.Identity,
+                scale=mix[:, s, j : j + 1], bias=bias_mix[:, s, j : j + 1],
+            )
+
+        def tile_transposes(t):
+            u, i = divmod(t, GROUP_TILES)
+            sup_tile = psum_sup.tile([P, Q], F32, name="sup")
+            for j in range(Q_SLICES):
+                nc.tensor.transpose(
+                    sup_tile[:, j * P : (j + 1) * P], sup_t[u][:, j, i * P : (i + 1) * P], ident[:]
+                )
+            sup[t] = sup_tile
+
+        def tile_halves(t):
+            halves_t = stat_pool.tile([P, 6], F32, name="halves")
+            nc.vector.bn_stats(out=halves_t[:], in_=sup[t][:])
+            halves[t] = halves_t
+
+        def tile_mean_var(t):
+            u, i = divmod(t, GROUP_TILES)
+            if i == 0:
+                mean_var_u = stat_pool.tile([P, GROUP_TILES, 2], F32, name="mean_var")
+                mean_var[u] = mean_var_u
+            nc.vector.bn_aggr(out=mean_var[u][:, i, :], in_=halves[t][:])
+
+        def tile_centre_and_gain(t):
+            u, i = divmod(t, GROUP_TILES)
+            y_t = y_pool.tile([P, Q], F32, name="y")
+            nc.vector.scalar_tensor_tensor(
+                out=y_t[:], in0=sup[t][:], scalar=mean_var[u][:, i, 0:1], in1=gain,
+                op0=ALU.subtract, op1=ALU.mult,
+            )
+            y[t] = y_t
+
+        def unit_rstd(u):
+            rstd_u = stat_pool.tile([P, GROUP_TILES], F32, name="rstd")
+            nc.scalar.activation(
+                out=rstd_u[:], in_=mean_var[u][:, :, 1], func=ACT.Abs_reciprocal_sqrt,
+                bias=eps[:, 0:1], scale=1.0,
+            )
+            rstd[u] = rstd_u
+
+        def tile_finish(t):
+            u, i = divmod(t, GROUP_TILES)
+            g, s = divmod(u, STATES)
+            if u < UNITS - 1:
+                nc.scalar.activation(
+                    out=y[t][:], in_=y[t][:], func=ACT.Copy, scale=rstd[u][:, i : i + 1]
+                )
+                nc.gpsimd.tensor_tensor(out=y[t][:], in0=y[t][:], in1=shift, op=ALU.add)
+            else:
+                nc.vector.scalar_tensor_tensor(
+                    out=y[t][:], in0=y[t][:], scalar=rstd[u][:, i : i + 1], in1=shift,
+                    op0=ALU.mult, op1=ALU.add,
+                )
+            nc.sync.dma_start(out=out_view[:, g * GROUP_TILES + i, s, :], in_=y[t][:])
+
+        for t in range(-2 * GROUP_TILES, TILES + LAG):
+            u, i = divmod(t, GROUP_TILES)
+            ahead = u + 2
+            if i == LAG and 0 <= u < UNITS:
+                unit_rstd(u)
+            if ahead < UNITS:
+                slice_products(ahead, i)
+            g_next = ahead // STATES + 1
+            pair = ahead % STATES - 1
+            if g_next < GROUPS and pair >= 0:
+                if i == 0:
+                    x_transposes(g_next, pair)
+                if i == 1:
+                    x_regroup(g_next, pair)
+                if i == 3 and pair == 1:
+                    x_quantise(g_next)
+            if ahead < UNITS:
+                slice_mix(ahead, i)
+            if 0 <= t + 1 < TILES:
+                tile_halves(t + 1)
+            if 0 <= t < TILES:
+                tile_centre_and_gain(t)
+            if 0 <= t + 1 < TILES:
+                tile_mean_var(t + 1)
+            if 0 <= t + GROUP_TILES < TILES:
+                tile_transposes(t + GROUP_TILES)
+            if 0 <= t - LAG:
+                tile_finish(t - LAG)

@@ -26,7 +26,11 @@ GROUPS = ROW_TILES // GROUP_TILES
 Q_SLICES = Q // P
 UNITS = GROUPS * STATES
 TILES = UNITS * GROUP_TILES
+SLICES = UNITS * Q_SLICES
+SUP_BANKS = 3
+LEAD = GROUP_TILES + SUP_BANKS
 LAG = GROUP_TILES - 1
+VECTOR_FINISHES = (1,)
 
 TWO_PI_HIGH = 6.28125
 TWO_PI_MID = 0.0019350051879882812
@@ -50,7 +54,8 @@ def tile_quantumsuperposition_t_kernel(
         y_pool = ctx.enter_context(tc.tile_pool(name="y", bufs=3 * GROUP_TILES))
         stat_pool = ctx.enter_context(tc.tile_pool(name="stat", bufs=4))
         psum_acc = ctx.enter_context(tc.psum_pool(name="psum_acc", bufs=3))
-        psum_sup = ctx.enter_context(tc.psum_pool(name="psum_sup", bufs=GROUP_TILES))
+        psum_sup = ctx.enter_context(tc.psum_pool(name="psum_sup", bufs=SUP_BANKS))
+        psum_shift = ctx.enter_context(tc.psum_pool(name="psum_shift", bufs=1))
         psum_x = ctx.enter_context(tc.psum_pool(name="psum_x", bufs=1))
         ctx.enter_context(tc.manual_schedule())
 
@@ -59,16 +64,21 @@ def tile_quantumsuperposition_t_kernel(
 
         vec_rows = consts.tile([P, P], BF16)
         nc.vector.memset(vec_rows[:], 0.0)
-        vec_count = STATES * Q_SLICES
-        for n, vec in enumerate((b, amplitude_weights, phase_weights)):
-            nc.scalar.dma_start(
-                out=vec_rows[n * vec_count : (n + 1) * vec_count, :],
+        per_vec = STATES * Q_SLICES
+        first_row = 0
+        for vec in (b, amplitude_weights, phase_weights):
+            nc.sync.dma_start(
+                out=vec_rows[first_row : first_row + per_vec, :],
                 in_=vec.rearrange("s (j p) -> (s j) p", p=P),
             )
-        gain_shift_row = consts.tile([P, 2, Q], BF16)
-        nc.vector.memset(gain_shift_row[:], 0.0)
-        nc.scalar.dma_start(out=gain_shift_row[0:1, 0, :], in_=ln_gamma.unsqueeze(0))
-        nc.scalar.dma_start(out=gain_shift_row[0:1, 1, :], in_=ln_beta.unsqueeze(0))
+            first_row += per_vec
+        for vec in (ln_gamma, ln_beta):
+            nc.sync.dma_start(
+                out=vec_rows[first_row : first_row + Q_SLICES, :],
+                in_=vec.rearrange("(j p) -> j p", p=P),
+            )
+            first_row += Q_SLICES
+        vec_columns = first_row
 
         w_rows = {}
         x_rows = {}
@@ -96,52 +106,61 @@ def tile_quantumsuperposition_t_kernel(
 
         ident = consts.tile([P, P], F32)
         make_identity(nc, ident[:])
-        ones = consts.tile([P, P], BF16)
-        nc.vector.memset(ones[:], 1.0)
         eps = consts.tile([P, 1], F32)
         nc.vector.memset(eps[:], LN_EPS)
+        warm_in = consts.tile([P, 1], F32)
+        nc.vector.memset(warm_in[:], 0.0)
+        warm_out = consts.tile([P, 1], F32)
+        nc.scalar.activation(out=warm_out[:], in_=warm_in[:], func=ACT.Exp)
 
         w_codes = consts.tile([P, STATES * Q], U32, align_bytes=64)
         w_scales = consts.tile([P, STATES * Q], U8, align_bytes=64)
+        w_grouped = {}
 
-        def quantise_w(s):
-            grouped = w_in.tile([P, Q * PACK], BF16, name="w_grouped", align_bytes=64)
+        def w_regroup(s, cols=slice(0, Q)):
+            grouped = w_in.tile([P, (cols.stop - cols.start) * PACK], BF16, name="w_grouped", align_bytes=64)
             nc.vector.tensor_copy(
                 out=grouped[:].rearrange("p (q t) -> p q t", t=PACK),
-                in_=w_rows[s][:].rearrange("p (t q) -> p q t", t=PACK),
+                in_=w_rows[s][:].rearrange("p (t q) -> p q t", t=PACK)[:, cols, :],
             )
+            w_grouped[s, cols.start] = grouped
+
+        def w_quantise(s, cols=slice(0, Q)):
+            codes = slice(s * Q + cols.start, s * Q + cols.stop)
             nc.vector.quantize_mx(
-                out=w_codes[:, s * Q : (s + 1) * Q].bitcast(FP8X4),
-                scales=w_scales[:, s * Q : (s + 1) * Q],
-                in_=grouped[:],
+                out=w_codes[:, codes].bitcast(FP8X4),
+                scales=w_scales[:, codes],
+                in_=w_grouped[s, cols.start][:],
             )
+
+        w_halves = (slice(0, Q // 2), slice(Q // 2, Q))
 
         x_t = {}
         x_grouped = {}
         x_codes = {}
         x_scales = {}
 
-        def x_transposes(g, pair):
+        def x_transposes(g, pair, bank):
             words = x_rows[g][:].bitcast(F32)
-            x_t_pair = psum_x.tile([P, 2, 2 * P], F32, tag="small")
             for ii in range(2):
                 for u in range(2):
                     first = (2 * pair + ii) * 2 * P
+                    column = (2 * u + ii) * P
                     nc.tensor.transpose(
-                        x_t_pair[:, u, ii * P : (ii + 1) * P],
+                        bank[:, column : column + P],
                         words[:, first + u : first + 2 * P : 2],
                         ident[:],
                     )
-            x_t[g, pair] = x_t_pair
+            x_t[g, pair] = bank
 
-        def x_regroup(g, pair):
+        def x_regroup(g, pair, copy):
             if pair == 0:
                 grouped = x_mx.tile([P, GROUP_ROWS * PACK], BF16, name="x_grouped", align_bytes=64)
                 x_grouped[g] = grouped
             grouped_words = x_grouped[g][:].bitcast(F32).rearrange("p (c u) -> p c u", u=2)
-            nc.scalar.copy(
+            copy(
                 out=grouped_words[:, pair * 2 * P : (pair + 1) * 2 * P, :],
-                in_=x_t[g, pair][:].rearrange("p u c -> p c u"),
+                in_=x_t[g, pair][:].rearrange("p (u c) -> p c u", u=2),
             )
 
         def x_quantise(g):
@@ -155,15 +174,17 @@ def tile_quantumsuperposition_t_kernel(
 
         vec_rows_f32 = consts.tile([P, P], F32)
         nc.vector.tensor_copy(out=vec_rows_f32[:], in_=vec_rows[:])
-        vec_t = psum_x.tile([P, P], F32, tag="small")
-        nc.tensor.transpose(vec_t[:], vec_rows_f32[:], ident[:])
-        vecs = consts.tile([P, 3, STATES, Q_SLICES], F32)
-        nc.vector.tensor_copy(
-            out=vecs[:].rearrange("p n s j -> p (n s j)"), in_=vec_t[:, 0 : 3 * vec_count]
-        )
-        bias = vecs[:, 0, :, :]
-        amplitude = vecs[:, 1, :, :]
-        phase = vecs[:, 2, :, :]
+        vec_t = psum_x.tile([P, Q], F32, name="small")
+        nc.tensor.transpose(vec_t[:, 0:P], vec_rows_f32[:], ident[:])
+        vecs = consts.tile([P, vec_columns], F32)
+        nc.vector.tensor_copy(out=vecs[:], in_=vec_t[:, 0:vec_columns])
+
+        def per_state_columns(n):
+            return vecs[:, n * per_vec : (n + 1) * per_vec].rearrange("p (s j) -> p s j", s=STATES)
+
+        bias = per_state_columns(0)
+        amplitude = per_state_columns(1)
+        phase = per_state_columns(2)
         per_state = [P, STATES, Q_SLICES]
 
         top = consts.tile([P, Q_SLICES], F32)
@@ -176,6 +197,10 @@ def tile_quantumsuperposition_t_kernel(
         )
         expd = consts.tile(per_state, F32)
         nc.scalar.activation(out=expd[:], in_=shifted[:], func=ACT.Exp)
+
+        for pair in range(2):
+            bank = psum_acc.tile([P, Q], F32, name="acc")
+            x_transposes(0, pair, bank)
 
         turns = consts.tile(per_state, F32)
         nc.vector.tensor_scalar(
@@ -198,47 +223,44 @@ def tile_quantumsuperposition_t_kernel(
         half_sin = consts.tile(per_state, F32)
         nc.scalar.activation(out=half_sin[:], in_=rest[:], func=ACT.Sin, scale=0.5)
 
-        gain_shift = consts.tile([P, 2, Q], F32)
-        for n in range(2):
-            spread = psum_acc.tile([P, Q], F32, name="acc")
-            nc.tensor.matmul(
-                out=spread[:], lhsT=ones[:], rhs=gain_shift_row[:, n, :], start=True, stop=True
-            )
-            nc.vector.tensor_copy(out=gain_shift[:, n, :], in_=spread[:])
-        gain = gain_shift[:, 0, :]
-        shift = gain_shift[:, 1, :]
+        x_regroup(0, 0, nc.scalar.copy)
+        x_regroup(0, 1, nc.vector.tensor_copy)
+        w_regroup(0, w_halves[0])
 
-        for pair in range(2):
-            x_transposes(0, pair)
-            x_regroup(0, pair)
-        quantise_w(0)
+        gain_bank = psum_sup.tile([P, Q], F32, name="sup")
+        shift_bank = psum_shift.tile([P, Q], F32, name="shift_bank")
+        for n, bank in enumerate((gain_bank, shift_bank)):
+            for j in range(Q_SLICES):
+                column = 3 * per_vec + n * Q_SLICES + j
+                nc.tensor.transpose(
+                    bank[:, j * P : (j + 1) * P],
+                    vecs[:, column : column + 1].to_broadcast([P, P]),
+                    ident[:],
+                )
+        gain = consts.tile([P, Q], F32)
+        shift = consts.tile([P, Q], F32)
 
+        x_quantise(0)
+        w_quantise(0, w_halves[0])
         total = consts.tile([P, Q_SLICES], F32)
         nc.vector.tensor_add(out=total[:], in0=expd[:, 0, :], in1=expd[:, 1, :])
         nc.vector.tensor_add(out=total[:], in0=total[:], in1=expd[:, 2, :])
         one_over_total = consts.tile([P, Q_SLICES], F32)
         nc.vector.reciprocal(out=one_over_total[:], in_=total[:])
+        amplitudes = consts.tile(per_state, F32)
+        nc.vector.tensor_mul(
+            out=amplitudes[:], in0=expd[:], in1=one_over_total[:].unsqueeze(1).to_broadcast(per_state)
+        )
         cosine = consts.tile(per_state, F32)
         nc.vector.tensor_mul(out=cosine[:], in0=half_sin[:], in1=half_sin[:])
         nc.vector.tensor_scalar(
             out=cosine[:], in0=cosine[:], scalar1=-2.0, scalar2=1.0, op0=ALU.mult, op1=ALU.add
         )
         mix = consts.tile(per_state, F32)
-        nc.vector.tensor_mul(out=mix[:], in0=expd[:], in1=cosine[:])
-        nc.vector.tensor_mul(
-            out=mix[:], in0=mix[:], in1=one_over_total[:].unsqueeze(1).to_broadcast(per_state)
-        )
+        nc.vector.tensor_mul(out=mix[:], in0=amplitudes[:], in1=cosine[:])
         bias_mix = consts.tile(per_state, F32)
         nc.vector.tensor_mul(out=bias_mix[:], in0=bias, in1=mix[:])
-
-        x_quantise(0)
-        quantise_w(1)
-        quantise_w(2)
-
-        table_warmer = consts.tile([P, 1], F32)
-        nc.scalar.activation(
-            out=table_warmer[:], in_=eps[:], func=ACT.Abs_reciprocal_sqrt, bias=eps[:, 0:1], scale=1.0
-        )
+        w_regroup(0, w_halves[1])
 
         acc = {}
         sup_t = {}
@@ -248,12 +270,13 @@ def tile_quantumsuperposition_t_kernel(
         rstd = {}
         y = {}
 
-        def slice_products(u, j):
+        def slice_products(e):
+            u, j = divmod(e, Q_SLICES)
             g, s = divmod(u, STATES)
             cols = slice(s * Q + j * P, s * Q + (j + 1) * P)
-            acc_j = psum_acc.tile([P, GROUP_ROWS], F32, name="acc")
+            acc_e = psum_acc.tile([P, GROUP_ROWS], F32, name="acc")
             nc.tensor.matmul_mx(
-                out=acc_j[:],
+                out=acc_e[:],
                 lhsT=w_codes[:, cols].bitcast(FP8X4),
                 lhsT_scale=w_scales[:, cols],
                 rhs=x_codes[g][:].bitcast(FP8X4),
@@ -261,17 +284,25 @@ def tile_quantumsuperposition_t_kernel(
                 start=True,
                 stop=True,
             )
-            acc[u, j] = acc_j
+            acc[e] = acc_e
 
-        def slice_mix(u, j):
+        def slice_mix(e):
+            u, j = divmod(e, Q_SLICES)
             s = u % STATES
             if j == 0:
                 sup_t_u = sup_t_pool.tile([P, Q_SLICES, GROUP_ROWS], F32, name="sup_t")
                 sup_t[u] = sup_t_u
-            nc.scalar.activation(
-                out=sup_t[u][:, j, :], in_=acc[u, j][:], func=ACT.Identity,
-                scale=mix[:, s, j : j + 1], bias=bias_mix[:, s, j : j + 1],
-            )
+            if e < Q_SLICES and j % 2 == 1:
+                nc.vector.tensor_scalar(
+                    out=sup_t[u][:, j, :], in0=acc[e][:],
+                    scalar1=mix[:, s, j : j + 1], scalar2=bias_mix[:, s, j : j + 1],
+                    op0=ALU.mult, op1=ALU.add,
+                )
+            else:
+                nc.scalar.activation(
+                    out=sup_t[u][:, j, :], in_=acc[e][:], func=ACT.Identity,
+                    scale=mix[:, s, j : j + 1], bias=bias_mix[:, s, j : j + 1],
+                )
 
         def tile_transposes(t):
             u, i = divmod(t, GROUP_TILES)
@@ -298,7 +329,7 @@ def tile_quantumsuperposition_t_kernel(
             u, i = divmod(t, GROUP_TILES)
             y_t = y_pool.tile([P, Q], F32, name="y")
             nc.vector.scalar_tensor_tensor(
-                out=y_t[:], in0=sup[t][:], scalar=mean_var[u][:, i, 0:1], in1=gain,
+                out=y_t[:], in0=sup[t][:], scalar=mean_var[u][:, i, 0:1], in1=gain[:],
                 op0=ALU.subtract, op1=ALU.mult,
             )
             y[t] = y_t
@@ -314,43 +345,61 @@ def tile_quantumsuperposition_t_kernel(
         def tile_finish(t):
             u, i = divmod(t, GROUP_TILES)
             g, s = divmod(u, STATES)
-            if u < UNITS - 1:
+            if i in VECTOR_FINISHES or u == UNITS - 1:
+                nc.vector.scalar_tensor_tensor(
+                    out=y[t][:], in0=y[t][:], scalar=rstd[u][:, i : i + 1], in1=shift_bank[:],
+                    op0=ALU.mult, op1=ALU.add,
+                )
+            else:
                 nc.scalar.activation(
                     out=y[t][:], in_=y[t][:], func=ACT.Copy, scale=rstd[u][:, i : i + 1]
                 )
-                nc.gpsimd.tensor_tensor(out=y[t][:], in0=y[t][:], in1=shift, op=ALU.add)
-            else:
-                nc.vector.scalar_tensor_tensor(
-                    out=y[t][:], in0=y[t][:], scalar=rstd[u][:, i : i + 1], in1=shift,
-                    op0=ALU.mult, op1=ALU.add,
-                )
+                nc.gpsimd.tensor_tensor(out=y[t][:], in0=y[t][:], in1=shift[:], op=ALU.add)
             nc.sync.dma_start(out=out_view[:, g * GROUP_TILES + i, s, :], in_=y[t][:])
 
-        for t in range(-2 * GROUP_TILES, TILES + LAG):
+        slice_products(0)
+        slice_products(1)
+        w_quantise(0, w_halves[1])
+        for t in range(-LEAD, TILES + LAG):
             u, i = divmod(t, GROUP_TILES)
-            ahead = u + 2
+            e = t + LEAD
             if i == LAG and 0 <= u < UNITS:
                 unit_rstd(u)
-            if ahead < UNITS:
-                slice_products(ahead, i)
+            if 1 < e + 1 < SLICES:
+                slice_products(e + 1)
+            ahead, j = divmod(e, Q_SLICES)
             g_next = ahead // STATES + 1
             pair = ahead % STATES - 1
             if g_next < GROUPS and pair >= 0:
-                if i == 0:
-                    x_transposes(g_next, pair)
-                if i == 1:
-                    x_regroup(g_next, pair)
-                if i == 3 and pair == 1:
+                if j == 0:
+                    bank = psum_x.tile([P, Q], F32, name="small")
+                    x_transposes(g_next, pair, bank)
+                if j == 1:
+                    x_regroup(g_next, pair, nc.scalar.copy)
+                if j == 2 and pair == 1:
                     x_quantise(g_next)
-            if ahead < UNITS:
-                slice_mix(ahead, i)
+            if e < SLICES:
+                slice_mix(e)
+            if e == 1:
+                w_regroup(1)
+                nc.vector.tensor_copy(out=gain[:], in_=gain_bank[:])
+                w_quantise(1)
+            if e == 3:
+                nc.vector.tensor_copy(out=shift[:], in_=shift_bank[:])
+                nc.scalar.activation(
+                    out=warm_out[:], in_=eps[:], func=ACT.Abs_reciprocal_sqrt, bias=eps[:, 0:1], scale=1.0
+                )
+            if e == 5:
+                w_regroup(2)
+            if e == 6:
+                w_quantise(2)
             if 0 <= t + 1 < TILES:
                 tile_halves(t + 1)
             if 0 <= t < TILES:
                 tile_centre_and_gain(t)
             if 0 <= t + 1 < TILES:
                 tile_mean_var(t + 1)
-            if 0 <= t + GROUP_TILES < TILES:
-                tile_transposes(t + GROUP_TILES)
+            if 0 <= t + SUP_BANKS < TILES:
+                tile_transposes(t + SUP_BANKS)
             if 0 <= t - LAG:
                 tile_finish(t - LAG)

@@ -27,10 +27,9 @@ Q_SLICES = Q // P
 UNITS = GROUPS * STATES
 TILES = UNITS * GROUP_TILES
 SLICES = UNITS * Q_SLICES
-SUP_BANKS = 3
-LEAD = GROUP_TILES + SUP_BANKS
+SUP_BANKS = 4
+LEAD = GROUP_TILES + SUP_BANKS - 1
 LAG = GROUP_TILES - 1
-VECTOR_FINISHES = (1,)
 
 TWO_PI_HIGH = 6.28125
 TWO_PI_MID = 0.0019350051879882812
@@ -55,7 +54,6 @@ def tile_quantumsuperposition_t_kernel(
         stat_pool = ctx.enter_context(tc.tile_pool(name="stat", bufs=4))
         psum_acc = ctx.enter_context(tc.psum_pool(name="psum_acc", bufs=3))
         psum_sup = ctx.enter_context(tc.psum_pool(name="psum_sup", bufs=SUP_BANKS))
-        psum_shift = ctx.enter_context(tc.psum_pool(name="psum_shift", bufs=1))
         psum_x = ctx.enter_context(tc.psum_pool(name="psum_x", bufs=1))
         ctx.enter_context(tc.manual_schedule())
 
@@ -66,14 +64,14 @@ def tile_quantumsuperposition_t_kernel(
         nc.vector.memset(vec_rows[:], 0.0)
         per_vec = STATES * Q_SLICES
         first_row = 0
-        for vec in (b, amplitude_weights, phase_weights):
-            nc.sync.dma_start(
+        for queue, vec in ((nc.sync, phase_weights), (nc.sync, amplitude_weights), (nc.scalar, b)):
+            queue.dma_start(
                 out=vec_rows[first_row : first_row + per_vec, :],
                 in_=vec.rearrange("s (j p) -> (s j) p", p=P),
             )
             first_row += per_vec
         for vec in (ln_gamma, ln_beta):
-            nc.sync.dma_start(
+            nc.scalar.dma_start(
                 out=vec_rows[first_row : first_row + Q_SLICES, :],
                 in_=vec.rearrange("(j p) -> j p", p=P),
             )
@@ -182,10 +180,40 @@ def tile_quantumsuperposition_t_kernel(
         def per_state_columns(n):
             return vecs[:, n * per_vec : (n + 1) * per_vec].rearrange("p (s j) -> p s j", s=STATES)
 
-        bias = per_state_columns(0)
+        phase = per_state_columns(0)
         amplitude = per_state_columns(1)
-        phase = per_state_columns(2)
+        bias = per_state_columns(2)
         per_state = [P, STATES, Q_SLICES]
+
+        spread_banks = []
+        for n in range(2):
+            bank = psum_sup.tile([P, Q], F32, name="sup")
+            for j in range(Q_SLICES):
+                column = 3 * per_vec + n * Q_SLICES + j
+                nc.tensor.transpose(
+                    bank[:, j * P : (j + 1) * P],
+                    vecs[:, column : column + 1].to_broadcast([P, P]),
+                    ident[:],
+                )
+            spread_banks.append(bank)
+
+        turns = consts.tile(per_state, F32)
+        nc.gpsimd.tensor_scalar(
+            out=turns[:], in0=phase, scalar1=ONE_OVER_TWO_PI, scalar2=ROUND_TO_WHOLE,
+            op0=ALU.mult, op1=ALU.add,
+        )
+        nc.gpsimd.tensor_scalar(
+            out=turns[:], in0=turns[:], scalar1=ROUND_TO_WHOLE, scalar2=0.0,
+            op0=ALU.subtract, op1=ALU.add,
+        )
+        rest = consts.tile(per_state, F32)
+        nc.gpsimd.tensor_copy(out=rest[:], in_=phase)
+        for part in (TWO_PI_HIGH, TWO_PI_MID, TWO_PI_LOW):
+            taken = consts.tile(per_state, F32, name="taken")
+            nc.gpsimd.tensor_scalar(
+                out=taken[:], in0=turns[:], scalar1=part, scalar2=0.0, op0=ALU.mult, op1=ALU.add
+            )
+            nc.gpsimd.tensor_tensor(out=rest[:], in0=rest[:], in1=taken[:], op=ALU.subtract)
 
         top = consts.tile([P, Q_SLICES], F32)
         nc.vector.tensor_max(out=top[:], in0=amplitude[:, 0, :], in1=amplitude[:, 1, :])
@@ -197,70 +225,40 @@ def tile_quantumsuperposition_t_kernel(
         )
         expd = consts.tile(per_state, F32)
         nc.scalar.activation(out=expd[:], in_=shifted[:], func=ACT.Exp)
-
         for pair in range(2):
             bank = psum_acc.tile([P, Q], F32, name="acc")
             x_transposes(0, pair, bank)
-
-        turns = consts.tile(per_state, F32)
-        nc.vector.tensor_scalar(
-            out=turns[:], in0=phase, scalar1=ONE_OVER_TWO_PI, scalar2=ROUND_TO_WHOLE,
-            op0=ALU.mult, op1=ALU.add,
-        )
-        nc.vector.tensor_scalar_sub(out=turns[:], in0=turns[:], scalar1=ROUND_TO_WHOLE)
-        rest_a = consts.tile(per_state, F32)
-        nc.vector.scalar_tensor_tensor(
-            out=rest_a[:], in0=turns[:], scalar=-TWO_PI_HIGH, in1=phase, op0=ALU.mult, op1=ALU.add
-        )
-        rest_b = consts.tile(per_state, F32)
-        nc.vector.scalar_tensor_tensor(
-            out=rest_b[:], in0=turns[:], scalar=-TWO_PI_MID, in1=rest_a[:], op0=ALU.mult, op1=ALU.add
-        )
-        rest = consts.tile(per_state, F32)
-        nc.vector.scalar_tensor_tensor(
-            out=rest[:], in0=turns[:], scalar=-TWO_PI_LOW, in1=rest_b[:], op0=ALU.mult, op1=ALU.add
-        )
+        x_regroup(0, 0, nc.scalar.copy)
         half_sin = consts.tile(per_state, F32)
         nc.scalar.activation(out=half_sin[:], in_=rest[:], func=ACT.Sin, scale=0.5)
-
-        x_regroup(0, 0, nc.scalar.copy)
+        gain = consts.tile([P, Q], F32)
+        nc.scalar.copy(out=gain[:], in_=spread_banks[0][:])
+        shift = consts.tile([P, Q], F32)
+        nc.scalar.copy(out=shift[:], in_=spread_banks[1][:])
         x_regroup(0, 1, nc.vector.tensor_copy)
         w_regroup(0, w_halves[0])
-
-        gain_bank = psum_sup.tile([P, Q], F32, name="sup")
-        shift_bank = psum_shift.tile([P, Q], F32, name="shift_bank")
-        for n, bank in enumerate((gain_bank, shift_bank)):
-            for j in range(Q_SLICES):
-                column = 3 * per_vec + n * Q_SLICES + j
-                nc.tensor.transpose(
-                    bank[:, j * P : (j + 1) * P],
-                    vecs[:, column : column + 1].to_broadcast([P, P]),
-                    ident[:],
-                )
-        gain = consts.tile([P, Q], F32)
-        shift = consts.tile([P, Q], F32)
-
-        x_quantise(0)
-        w_quantise(0, w_halves[0])
         total = consts.tile([P, Q_SLICES], F32)
         nc.vector.tensor_add(out=total[:], in0=expd[:, 0, :], in1=expd[:, 1, :])
+        x_quantise(0)
         nc.vector.tensor_add(out=total[:], in0=total[:], in1=expd[:, 2, :])
+        w_quantise(0, w_halves[0])
         one_over_total = consts.tile([P, Q_SLICES], F32)
         nc.vector.reciprocal(out=one_over_total[:], in_=total[:])
-        amplitudes = consts.tile(per_state, F32)
-        nc.vector.tensor_mul(
-            out=amplitudes[:], in0=expd[:], in1=one_over_total[:].unsqueeze(1).to_broadcast(per_state)
-        )
+        w_regroup(0, w_halves[1])
+
         cosine = consts.tile(per_state, F32)
-        nc.vector.tensor_mul(out=cosine[:], in0=half_sin[:], in1=half_sin[:])
-        nc.vector.tensor_scalar(
+        nc.gpsimd.tensor_tensor(out=cosine[:], in0=half_sin[:], in1=half_sin[:], op=ALU.mult)
+        nc.gpsimd.tensor_scalar(
             out=cosine[:], in0=cosine[:], scalar1=-2.0, scalar2=1.0, op0=ALU.mult, op1=ALU.add
         )
         mix = consts.tile(per_state, F32)
-        nc.vector.tensor_mul(out=mix[:], in0=amplitudes[:], in1=cosine[:])
+        nc.gpsimd.tensor_tensor(out=mix[:], in0=expd[:], in1=cosine[:], op=ALU.mult)
+        nc.gpsimd.tensor_tensor(
+            out=mix[:], in0=mix[:], in1=one_over_total[:].unsqueeze(1).to_broadcast(per_state),
+            op=ALU.mult,
+        )
         bias_mix = consts.tile(per_state, F32)
-        nc.vector.tensor_mul(out=bias_mix[:], in0=bias, in1=mix[:])
-        w_regroup(0, w_halves[1])
+        nc.gpsimd.tensor_tensor(out=bias_mix[:], in0=bias, in1=mix[:], op=ALU.mult)
 
         acc = {}
         sup_t = {}
@@ -286,13 +284,25 @@ def tile_quantumsuperposition_t_kernel(
             )
             acc[e] = acc_e
 
+        def keep_clock_up(g):
+            idle = psum_x.tile([P, Q], F32, name="small")
+            nc.tensor.matmul_mx(
+                out=idle[:],
+                lhsT=w_codes[:, 0:P].bitcast(FP8X4),
+                lhsT_scale=w_scales[:, 0:P],
+                rhs=x_codes[g][:].bitcast(FP8X4),
+                rhs_scale=x_scales[g][:],
+                start=True,
+                stop=True,
+            )
+
         def slice_mix(e):
             u, j = divmod(e, Q_SLICES)
             s = u % STATES
             if j == 0:
                 sup_t_u = sup_t_pool.tile([P, Q_SLICES, GROUP_ROWS], F32, name="sup_t")
                 sup_t[u] = sup_t_u
-            if e < Q_SLICES and j % 2 == 1:
+            if e == 1:
                 nc.vector.tensor_scalar(
                     out=sup_t[u][:, j, :], in0=acc[e][:],
                     scalar1=mix[:, s, j : j + 1], scalar2=bias_mix[:, s, j : j + 1],
@@ -345,9 +355,9 @@ def tile_quantumsuperposition_t_kernel(
         def tile_finish(t):
             u, i = divmod(t, GROUP_TILES)
             g, s = divmod(u, STATES)
-            if i in VECTOR_FINISHES or u == UNITS - 1:
+            if u == UNITS - 1:
                 nc.vector.scalar_tensor_tensor(
-                    out=y[t][:], in0=y[t][:], scalar=rstd[u][:, i : i + 1], in1=shift_bank[:],
+                    out=y[t][:], in0=y[t][:], scalar=rstd[u][:, i : i + 1], in1=shift[:],
                     op0=ALU.mult, op1=ALU.add,
                 )
             else:
@@ -363,29 +373,34 @@ def tile_quantumsuperposition_t_kernel(
         for t in range(-LEAD, TILES + LAG):
             u, i = divmod(t, GROUP_TILES)
             e = t + LEAD
+            ahead, j = divmod(e, Q_SLICES)
+            g = ahead // STATES
             if i == LAG and 0 <= u < UNITS:
                 unit_rstd(u)
-            if 1 < e + 1 < SLICES:
+            if e == 3:
+                slice_mix(e)
+                tile_transposes(0)
+            if e % 2 == 1 and e + 2 < SLICES:
                 slice_products(e + 1)
-            ahead, j = divmod(e, Q_SLICES)
-            g_next = ahead // STATES + 1
-            pair = ahead % STATES - 1
-            if g_next < GROUPS and pair >= 0:
-                if j == 0:
+                slice_products(e + 2)
+                keep_clock_up(g)
+            if g + 1 < GROUPS:
+                if ahead % STATES == 1 and j % 2 == 1:
                     bank = psum_x.tile([P, Q], F32, name="small")
-                    x_transposes(g_next, pair, bank)
-                if j == 1:
-                    x_regroup(g_next, pair, nc.scalar.copy)
-                if j == 2 and pair == 1:
-                    x_quantise(g_next)
-            if e < SLICES:
+                    x_transposes(g + 1, j // 2, bank)
+                if ahead % STATES == 1 and j == 2:
+                    x_regroup(g + 1, 0, nc.scalar.copy)
+                if ahead % STATES == 2 and j == 0:
+                    x_regroup(g + 1, 1, nc.scalar.copy)
+                if ahead % STATES == 2 and j == 1:
+                    x_quantise(g + 1)
+            if e < SLICES and e != 3:
                 slice_mix(e)
             if e == 1:
                 w_regroup(1)
-                nc.vector.tensor_copy(out=gain[:], in_=gain_bank[:])
+            if e == 2:
                 w_quantise(1)
             if e == 3:
-                nc.vector.tensor_copy(out=shift[:], in_=shift_bank[:])
                 nc.scalar.activation(
                     out=warm_out[:], in_=eps[:], func=ACT.Abs_reciprocal_sqrt, bias=eps[:, 0:1], scale=1.0
                 )
@@ -399,7 +414,9 @@ def tile_quantumsuperposition_t_kernel(
                 tile_centre_and_gain(t)
             if 0 <= t + 1 < TILES:
                 tile_mean_var(t + 1)
-            if 0 <= t + SUP_BANKS < TILES:
-                tile_transposes(t + SUP_BANKS)
+            if t % 2 == 0:
+                for ahead_t in (t + SUP_BANKS - 1, t + SUP_BANKS):
+                    if 0 < ahead_t < TILES:
+                        tile_transposes(ahead_t)
             if 0 <= t - LAG:
                 tile_finish(t - LAG)

@@ -29,6 +29,10 @@ TILES = UNITS * GROUP_TILES
 SLICES = UNITS * Q_SLICES
 SUP_BANKS = 4
 LEAD = GROUP_TILES + SUP_BANKS - 1
+ADD_TILES = 2
+SINGLE_ADDS = TILES - 8
+SCALAR_STATISTICS = (TILES - 6, TILES - 4, TILES - 2)
+VECTOR_FINISHES = (TILES - 2, TILES - 1)
 LAG = GROUP_TILES - 1
 
 TWO_PI_HIGH = 6.28125
@@ -50,7 +54,8 @@ def tile_quantumsuperposition_t_kernel(
         x_mx = ctx.enter_context(tc.tile_pool(name="x_mx", bufs=2))
         w_in = ctx.enter_context(tc.tile_pool(name="w_in", bufs=STATES))
         sup_t_pool = ctx.enter_context(tc.tile_pool(name="sup_t", bufs=3))
-        y_pool = ctx.enter_context(tc.tile_pool(name="y", bufs=3 * GROUP_TILES))
+        tail_pool = ctx.enter_context(tc.tile_pool(name="tail", bufs=2))
+        y_pool = ctx.enter_context(tc.tile_pool(name="y", bufs=8))
         stat_pool = ctx.enter_context(tc.tile_pool(name="stat", bufs=4))
         psum_acc = ctx.enter_context(tc.psum_pool(name="psum_acc", bufs=3))
         psum_sup = ctx.enter_context(tc.psum_pool(name="psum_sup", bufs=SUP_BANKS))
@@ -81,23 +86,30 @@ def tile_quantumsuperposition_t_kernel(
         w_rows = {}
         x_rows = {}
 
-        def load_w(s):
+        def load_w(s, pieces=1):
             rows = w_in.tile([P, PACK * Q], BF16, name="w_rows")
-            nc.sync.dma_start(
-                out=rows[:], in_=W[s, :, :].rearrange("(p t) q -> p (t q)", t=PACK)
-            )
+            rows_view = rows[:].rearrange("p (t q) -> p t q", t=PACK)
+            w_view = W[s, :, :].rearrange("(p t) q -> p t q", t=PACK)
+            for n in range(pieces):
+                cols = slice(n * Q // pieces, (n + 1) * Q // pieces)
+                nc.sync.dma_start(out=rows_view[:, :, cols], in_=w_view[:, :, cols])
             w_rows[s] = rows
 
-        def load_x(g):
+        def load_x(g, pieces=1):
             rows = x_in.tile([P, GROUP_TILES * K], BF16, name="x_rows")
-            nc.sync.dma_start(
-                out=rows[:].rearrange("p (i k) -> p i k", i=GROUP_TILES),
-                in_=x_view[:, g * GROUP_TILES : (g + 1) * GROUP_TILES, :],
-            )
+            rows_view = rows[:].rearrange("p (i k) -> p i k", i=GROUP_TILES)
+            per_piece = GROUP_TILES // pieces
+            for n in range(pieces):
+                first = g * GROUP_TILES + n * per_piece
+                nc.sync.dma_start(
+                    out=rows_view[:, n * per_piece : (n + 1) * per_piece, :],
+                    in_=x_view[:, first : first + per_piece, :],
+                )
             x_rows[g] = rows
 
-        load_x(0)
-        for s in range(STATES):
+        load_x(0, pieces=2)
+        load_w(0, pieces=2)
+        for s in range(1, STATES):
             load_w(s)
         for g in range(1, GROUPS):
             load_x(g)
@@ -152,7 +164,7 @@ def tile_quantumsuperposition_t_kernel(
             x_t[g, pair] = bank
 
         def x_regroup(g, pair, copy):
-            if pair == 0:
+            if g not in x_grouped:
                 grouped = x_mx.tile([P, GROUP_ROWS * PACK], BF16, name="x_grouped", align_bytes=64)
                 x_grouped[g] = grouped
             grouped_words = x_grouped[g][:].bitcast(F32).rearrange("p (c u) -> p c u", u=2)
@@ -185,9 +197,7 @@ def tile_quantumsuperposition_t_kernel(
         bias = per_state_columns(2)
         per_state = [P, STATES, Q_SLICES]
 
-        spread_banks = []
-        for n in range(2):
-            bank = psum_sup.tile([P, Q], F32, name="sup")
+        def spread(n, bank):
             for j in range(Q_SLICES):
                 column = 3 * per_vec + n * Q_SLICES + j
                 nc.tensor.transpose(
@@ -195,7 +205,13 @@ def tile_quantumsuperposition_t_kernel(
                     vecs[:, column : column + 1].to_broadcast([P, P]),
                     ident[:],
                 )
+
+        spread_banks = []
+        for n in range(2):
+            bank = psum_sup.tile([P, Q], F32, name="sup")
+            spread(n, bank)
             spread_banks.append(bank)
+        shift_bank = []
 
         turns = consts.tile(per_state, F32)
         nc.gpsimd.tensor_scalar(
@@ -225,45 +241,48 @@ def tile_quantumsuperposition_t_kernel(
         )
         expd = consts.tile(per_state, F32)
         nc.scalar.activation(out=expd[:], in_=shifted[:], func=ACT.Exp)
+        half_sin = consts.tile(per_state, F32)
+        nc.scalar.activation(out=half_sin[:], in_=rest[:], func=ACT.Sin, scale=0.5)
+
         for pair in range(2):
             bank = psum_acc.tile([P, Q], F32, name="acc")
             x_transposes(0, pair, bank)
-        x_regroup(0, 0, nc.scalar.copy)
-        half_sin = consts.tile(per_state, F32)
-        nc.scalar.activation(out=half_sin[:], in_=rest[:], func=ACT.Sin, scale=0.5)
+        x_regroup(0, 1, nc.scalar.copy)
         gain = consts.tile([P, Q], F32)
         nc.scalar.copy(out=gain[:], in_=spread_banks[0][:])
         shift = consts.tile([P, Q], F32)
         nc.scalar.copy(out=shift[:], in_=spread_banks[1][:])
-        x_regroup(0, 1, nc.vector.tensor_copy)
-        w_regroup(0, w_halves[0])
+
         total = consts.tile([P, Q_SLICES], F32)
         nc.vector.tensor_add(out=total[:], in0=expd[:, 0, :], in1=expd[:, 1, :])
-        x_quantise(0)
         nc.vector.tensor_add(out=total[:], in0=total[:], in1=expd[:, 2, :])
-        w_quantise(0, w_halves[0])
         one_over_total = consts.tile([P, Q_SLICES], F32)
         nc.vector.reciprocal(out=one_over_total[:], in_=total[:])
-        w_regroup(0, w_halves[1])
-
+        x_regroup(0, 0, nc.vector.tensor_copy)
+        amplitudes = consts.tile(per_state, F32)
+        nc.vector.tensor_mul(
+            out=amplitudes[:], in0=expd[:], in1=one_over_total[:].unsqueeze(1).to_broadcast(per_state)
+        )
+        w_regroup(0, w_halves[0])
+        sin_squared = consts.tile(per_state, F32)
+        nc.vector.tensor_mul(out=sin_squared[:], in0=half_sin[:], in1=half_sin[:])
+        x_quantise(0)
         cosine = consts.tile(per_state, F32)
-        nc.gpsimd.tensor_tensor(out=cosine[:], in0=half_sin[:], in1=half_sin[:], op=ALU.mult)
-        nc.gpsimd.tensor_scalar(
-            out=cosine[:], in0=cosine[:], scalar1=-2.0, scalar2=1.0, op0=ALU.mult, op1=ALU.add
+        nc.vector.tensor_scalar(
+            out=cosine[:], in0=sin_squared[:], scalar1=-2.0, scalar2=1.0, op0=ALU.mult, op1=ALU.add
         )
+        w_quantise(0, w_halves[0])
         mix = consts.tile(per_state, F32)
-        nc.gpsimd.tensor_tensor(out=mix[:], in0=expd[:], in1=cosine[:], op=ALU.mult)
-        nc.gpsimd.tensor_tensor(
-            out=mix[:], in0=mix[:], in1=one_over_total[:].unsqueeze(1).to_broadcast(per_state),
-            op=ALU.mult,
-        )
+        nc.vector.tensor_mul(out=mix[:], in0=amplitudes[:], in1=cosine[:])
+        w_regroup(0, w_halves[1])
         bias_mix = consts.tile(per_state, F32)
-        nc.gpsimd.tensor_tensor(out=bias_mix[:], in0=bias, in1=mix[:], op=ALU.mult)
+        nc.vector.tensor_mul(out=bias_mix[:], in0=bias, in1=mix[:])
 
         acc = {}
         sup_t = {}
         sup = {}
         halves = {}
+        minus_mean = {}
         mean_var = {}
         rstd = {}
         y = {}
@@ -323,49 +342,90 @@ def tile_quantumsuperposition_t_kernel(
                 )
             sup[t] = sup_tile
 
+        def tile_statistics_on_scalar(t):
+            u, i = divmod(t, GROUP_TILES)
+            square = tail_pool.tile([P, Q], BF16, name="square")
+            row_sum = tail_pool.tile([P, 1], F32, name="row_sum")
+            nc.scalar.activation(out=square[:], in_=sup[t][:], func=ACT.Copy, accum_out=row_sum[:])
+            minus_mean_t = tail_pool.tile([P, 1], F32, name="minus_mean")
+            nc.scalar.activation(out=minus_mean_t[:], in_=row_sum[:], func=ACT.Copy, scale=-1.0 / Q)
+            minus_mean[t] = minus_mean_t
+            square_sum = tail_pool.tile([P, 1], F32, name="square_sum")
+            nc.scalar.activation(
+                out=square[:], in_=sup[t][:], func=ACT.Square, bias=minus_mean_t[:, 0:1],
+                scale=1.0, accum_out=square_sum[:],
+            )
+            nc.scalar.activation(
+                out=mean_var[u][:, i, 1:2], in_=square_sum[:], func=ACT.Copy, scale=1.0 / Q
+            )
+
         def tile_halves(t):
             halves_t = stat_pool.tile([P, 6], F32, name="halves")
             nc.vector.bn_stats(out=halves_t[:], in_=sup[t][:])
             halves[t] = halves_t
 
-        def tile_mean_var(t):
-            u, i = divmod(t, GROUP_TILES)
-            if i == 0:
+        def unit_statistics(u):
+            if u not in mean_var:
                 mean_var_u = stat_pool.tile([P, GROUP_TILES, 2], F32, name="mean_var")
                 mean_var[u] = mean_var_u
+
+        def tile_mean_var(t):
+            u, i = divmod(t, GROUP_TILES)
             nc.vector.bn_aggr(out=mean_var[u][:, i, :], in_=halves[t][:])
 
         def tile_centre_and_gain(t):
             u, i = divmod(t, GROUP_TILES)
-            y_t = y_pool.tile([P, Q], F32, name="y")
-            nc.vector.scalar_tensor_tensor(
-                out=y_t[:], in0=sup[t][:], scalar=mean_var[u][:, i, 0:1], in1=gain[:],
-                op0=ALU.subtract, op1=ALU.mult,
-            )
-            y[t] = y_t
+            if t % ADD_TILES == 0:
+                y_pair = y_pool.tile([P, ADD_TILES, Q], F32, name="y")
+                y[t // ADD_TILES] = y_pair
+            y_t = y[t // ADD_TILES][:, t % ADD_TILES, :]
+            if t in SCALAR_STATISTICS:
+                nc.vector.scalar_tensor_tensor(
+                    out=y_t, in0=sup[t][:], scalar=minus_mean[t][:, 0:1], in1=gain[:],
+                    op0=ALU.add, op1=ALU.mult,
+                )
+            else:
+                nc.vector.scalar_tensor_tensor(
+                    out=y_t, in0=sup[t][:], scalar=mean_var[u][:, i, 0:1], in1=gain[:],
+                    op0=ALU.subtract, op1=ALU.mult,
+                )
 
-        def unit_rstd(u):
-            rstd_u = stat_pool.tile([P, GROUP_TILES], F32, name="rstd")
+        def unit_rstd(u, tiles=slice(0, GROUP_TILES)):
+            if u not in rstd:
+                rstd_u = stat_pool.tile([P, GROUP_TILES], F32, name="rstd")
+                rstd[u] = rstd_u
             nc.scalar.activation(
-                out=rstd_u[:], in_=mean_var[u][:, :, 1], func=ACT.Abs_reciprocal_sqrt,
+                out=rstd[u][:, tiles], in_=mean_var[u][:, tiles, 1], func=ACT.Abs_reciprocal_sqrt,
                 bias=eps[:, 0:1], scale=1.0,
             )
-            rstd[u] = rstd_u
 
         def tile_finish(t):
             u, i = divmod(t, GROUP_TILES)
             g, s = divmod(u, STATES)
-            if u == UNITS - 1:
+            pair = y[t // ADD_TILES]
+            n = t % ADD_TILES
+            tile_rstd = rstd[u][:, i : i + 1]
+            if t in VECTOR_FINISHES:
                 nc.vector.scalar_tensor_tensor(
-                    out=y[t][:], in0=y[t][:], scalar=rstd[u][:, i : i + 1], in1=shift[:],
+                    out=pair[:, n, :], in0=pair[:, n, :], scalar=tile_rstd, in1=shift_bank[0][:],
                     op0=ALU.mult, op1=ALU.add,
                 )
+                tiles = slice(n, n + 1)
             else:
                 nc.scalar.activation(
-                    out=y[t][:], in_=y[t][:], func=ACT.Copy, scale=rstd[u][:, i : i + 1]
+                    out=pair[:, n, :], in_=pair[:, n, :], func=ACT.Copy, scale=tile_rstd
                 )
-                nc.gpsimd.tensor_tensor(out=y[t][:], in0=y[t][:], in1=shift[:], op=ALU.add)
-            nc.sync.dma_start(out=out_view[:, g * GROUP_TILES + i, s, :], in_=y[t][:])
+                if t < SINGLE_ADDS and n < ADD_TILES - 1:
+                    return
+                tiles = slice(n, n + 1) if t >= SINGLE_ADDS else slice(0, ADD_TILES)
+                per_add = tiles.stop - tiles.start
+                nc.gpsimd.tensor_tensor(
+                    out=pair[:, tiles, :], in0=pair[:, tiles, :],
+                    in1=shift[:].unsqueeze(1).to_broadcast([P, per_add, Q]), op=ALU.add,
+                )
+            first = g * GROUP_TILES + i + tiles.start - n
+            last = g * GROUP_TILES + i + tiles.stop - n
+            nc.sync.dma_start(out=out_view[:, first:last, s, :], in_=pair[:, tiles, :])
 
         slice_products(0)
         slice_products(1)
@@ -375,11 +435,16 @@ def tile_quantumsuperposition_t_kernel(
             e = t + LEAD
             ahead, j = divmod(e, Q_SLICES)
             g = ahead // STATES
-            if i == LAG and 0 <= u < UNITS:
+            if 0 <= t + 1 < TILES:
+                unit_statistics((t + 1) // GROUP_TILES)
+            if i == LAG and 0 <= u < UNITS - 1:
                 unit_rstd(u)
             if e == 3:
                 slice_mix(e)
-                tile_transposes(0)
+                for first in range(GROUP_TILES):
+                    tile_transposes(first)
+            if t == 0:
+                w_quantise(2)
             if e % 2 == 1 and e + 2 < SLICES:
                 slice_products(e + 1)
                 slice_products(e + 2)
@@ -388,14 +453,10 @@ def tile_quantumsuperposition_t_kernel(
                 if ahead % STATES == 1 and j % 2 == 1:
                     bank = psum_x.tile([P, Q], F32, name="small")
                     x_transposes(g + 1, j // 2, bank)
-                if ahead % STATES == 1 and j == 2:
-                    x_regroup(g + 1, 0, nc.scalar.copy)
-                if ahead % STATES == 2 and j == 0:
-                    x_regroup(g + 1, 1, nc.scalar.copy)
-                if ahead % STATES == 2 and j == 1:
-                    x_quantise(g + 1)
             if e < SLICES and e != 3:
                 slice_mix(e)
+            if g + 1 < GROUPS and ahead % STATES == 1 and j == 2:
+                x_regroup(g + 1, 0, nc.scalar.copy)
             if e == 1:
                 w_regroup(1)
             if e == 2:
@@ -404,19 +465,35 @@ def tile_quantumsuperposition_t_kernel(
                 nc.scalar.activation(
                     out=warm_out[:], in_=eps[:], func=ACT.Abs_reciprocal_sqrt, bias=eps[:, 0:1], scale=1.0
                 )
-            if e == 5:
-                w_regroup(2)
-            if e == 6:
-                w_quantise(2)
-            if 0 <= t + 1 < TILES:
+            if t + 1 in SCALAR_STATISTICS:
+                tile_statistics_on_scalar(t + 1)
+            elif 0 <= t + 1 < TILES:
                 tile_halves(t + 1)
+            if t == -1:
+                w_regroup(2)
+            if g + 1 < GROUPS and ahead % STATES == 2 and j == 1:
+                x_regroup(g + 1, 1, nc.vector.tensor_copy)
+            if g + 1 < GROUPS and ahead % STATES == 2 and j == 2:
+                x_quantise(g + 1)
             if 0 <= t < TILES:
                 tile_centre_and_gain(t)
-            if 0 <= t + 1 < TILES:
+            if 0 <= t + 1 < TILES and t + 1 not in SCALAR_STATISTICS:
                 tile_mean_var(t + 1)
             if t % 2 == 0:
                 for ahead_t in (t + SUP_BANKS - 1, t + SUP_BANKS):
-                    if 0 < ahead_t < TILES:
+                    if GROUP_TILES <= ahead_t < TILES:
                         tile_transposes(ahead_t)
-            if 0 <= t - LAG:
+            if t == TILES - LEAD + 2:
+                bank = psum_acc.tile([P, Q], F32, name="acc")
+                spread(1, bank)
+                shift_bank.append(bank)
+            if t == TILES - 2:
+                unit_rstd(UNITS - 1, slice(0, 2))
+                for last in range(TILES - 5, TILES - 2):
+                    tile_finish(last)
+            elif t == TILES - 1:
+                unit_rstd(UNITS - 1, slice(2, 4))
+                for last in VECTOR_FINISHES:
+                    tile_finish(last)
+            elif 0 <= t - LAG and t < TILES - 2:
                 tile_finish(t - LAG)

@@ -68,20 +68,16 @@ def tile_quantumsuperposition_t_kernel(
         vec_rows = consts.tile([P, P], BF16)
         nc.vector.memset(vec_rows[:], 0.0)
         per_vec = STATES * Q_SLICES
-        first_row = 0
-        for queue, vec in ((nc.sync, phase_weights), (nc.sync, amplitude_weights), (nc.scalar, b)):
-            queue.dma_start(
-                out=vec_rows[first_row : first_row + per_vec, :],
-                in_=vec.rearrange("s (j p) -> (s j) p", p=P),
-            )
-            first_row += per_vec
-        for vec in (ln_gamma, ln_beta):
-            nc.scalar.dma_start(
-                out=vec_rows[first_row : first_row + Q_SLICES, :],
-                in_=vec.rearrange("(j p) -> j p", p=P),
-            )
-            first_row += Q_SLICES
-        vec_columns = first_row
+        vec_columns = 3 * per_vec + 2 * Q_SLICES
+
+        def load_vec(queue, vec, first_row, rows):
+            queue.dma_start(out=vec_rows[first_row : first_row + rows, :], in_=vec)
+
+        load_vec(nc.scalar, b.rearrange("s (j p) -> (s j) p", p=P), 2 * per_vec, per_vec)
+        load_vec(nc.scalar, ln_gamma.rearrange("(j p) -> j p", p=P), 3 * per_vec, Q_SLICES)
+        load_vec(
+            nc.scalar, ln_beta.rearrange("(j p) -> j p", p=P), 3 * per_vec + Q_SLICES, Q_SLICES
+        )
 
         w_rows = {}
         x_rows = {}
@@ -95,19 +91,21 @@ def tile_quantumsuperposition_t_kernel(
                 nc.sync.dma_start(out=rows_view[:, :, cols], in_=w_view[:, :, cols])
             w_rows[s] = rows
 
-        def load_x(g, pieces=1):
-            rows = x_in.tile([P, GROUP_TILES * K], BF16, name="x_rows")
-            rows_view = rows[:].rearrange("p (i k) -> p i k", i=GROUP_TILES)
-            per_piece = GROUP_TILES // pieces
-            for n in range(pieces):
-                first = g * GROUP_TILES + n * per_piece
-                nc.sync.dma_start(
-                    out=rows_view[:, n * per_piece : (n + 1) * per_piece, :],
-                    in_=x_view[:, first : first + per_piece, :],
-                )
-            x_rows[g] = rows
+        def load_x(g, tiles=slice(0, GROUP_TILES)):
+            if g not in x_rows:
+                rows = x_in.tile([P, GROUP_TILES * K], BF16, name="x_rows")
+                x_rows[g] = rows
+            rows_view = x_rows[g][:].rearrange("p (i k) -> p i k", i=GROUP_TILES)
+            first = g * GROUP_TILES
+            nc.sync.dma_start(
+                out=rows_view[:, tiles, :],
+                in_=x_view[:, first + tiles.start : first + tiles.stop, :],
+            )
 
-        load_x(0, pieces=2)
+        load_x(0, slice(0, 2))
+        load_vec(nc.sync, phase_weights.rearrange("s (j p) -> (s j) p", p=P), 0, per_vec)
+        load_vec(nc.sync, amplitude_weights.rearrange("s (j p) -> (s j) p", p=P), per_vec, per_vec)
+        load_x(0, slice(2, 4))
         load_w(0, pieces=2)
         for s in range(1, STATES):
             load_w(s)
@@ -182,6 +180,12 @@ def tile_quantumsuperposition_t_kernel(
             x_codes[g] = codes
             x_scales[g] = scales
 
+        def first_rows(pair, copy):
+            bank = psum_acc.tile([P, Q], F32, name="acc")
+            x_transposes(0, pair, bank)
+            x_regroup(0, pair, copy)
+
+        first_rows(0, nc.scalar.copy)
         vec_rows_f32 = consts.tile([P, P], F32)
         nc.vector.tensor_copy(out=vec_rows_f32[:], in_=vec_rows[:])
         vec_t = psum_x.tile([P, Q], F32, name="small")
@@ -206,11 +210,6 @@ def tile_quantumsuperposition_t_kernel(
                     ident[:],
                 )
 
-        spread_banks = []
-        for n in range(2):
-            bank = psum_sup.tile([P, Q], F32, name="sup")
-            spread(n, bank)
-            spread_banks.append(bank)
         shift_bank = []
 
         turns = consts.tile(per_state, F32)
@@ -244,45 +243,46 @@ def tile_quantumsuperposition_t_kernel(
         half_sin = consts.tile(per_state, F32)
         nc.scalar.activation(out=half_sin[:], in_=rest[:], func=ACT.Sin, scale=0.5)
 
-        for pair in range(2):
-            bank = psum_acc.tile([P, Q], F32, name="acc")
-            x_transposes(0, pair, bank)
-        x_regroup(0, 1, nc.scalar.copy)
+        first_rows(1, nc.vector.tensor_copy)
+        spread_banks = []
+        for n in range(2):
+            bank = psum_sup.tile([P, Q], F32, name="sup")
+            spread(n, bank)
+            spread_banks.append(bank)
         gain = consts.tile([P, Q], F32)
-        nc.scalar.copy(out=gain[:], in_=spread_banks[0][:])
         shift = consts.tile([P, Q], F32)
-        nc.scalar.copy(out=shift[:], in_=spread_banks[1][:])
 
+        w_regroup(0, w_halves[0])
         total = consts.tile([P, Q_SLICES], F32)
         nc.vector.tensor_add(out=total[:], in0=expd[:, 0, :], in1=expd[:, 1, :])
+        x_quantise(0)
         nc.vector.tensor_add(out=total[:], in0=total[:], in1=expd[:, 2, :])
+        w_quantise(0, w_halves[0])
         one_over_total = consts.tile([P, Q_SLICES], F32)
         nc.vector.reciprocal(out=one_over_total[:], in_=total[:])
-        x_regroup(0, 0, nc.vector.tensor_copy)
+        sin_squared = consts.tile(per_state, F32)
+        nc.vector.tensor_mul(out=sin_squared[:], in0=half_sin[:], in1=half_sin[:])
         amplitudes = consts.tile(per_state, F32)
         nc.vector.tensor_mul(
             out=amplitudes[:], in0=expd[:], in1=one_over_total[:].unsqueeze(1).to_broadcast(per_state)
         )
-        w_regroup(0, w_halves[0])
-        sin_squared = consts.tile(per_state, F32)
-        nc.vector.tensor_mul(out=sin_squared[:], in0=half_sin[:], in1=half_sin[:])
-        x_quantise(0)
         cosine = consts.tile(per_state, F32)
         nc.vector.tensor_scalar(
             out=cosine[:], in0=sin_squared[:], scalar1=-2.0, scalar2=1.0, op0=ALU.mult, op1=ALU.add
         )
-        w_quantise(0, w_halves[0])
         mix = consts.tile(per_state, F32)
         nc.vector.tensor_mul(out=mix[:], in0=amplitudes[:], in1=cosine[:])
-        w_regroup(0, w_halves[1])
         bias_mix = consts.tile(per_state, F32)
         nc.vector.tensor_mul(out=bias_mix[:], in0=bias, in1=mix[:])
+        w_regroup(0, w_halves[1])
 
         acc = {}
         sup_t = {}
         sup = {}
         halves = {}
+        row_sum = {}
         minus_mean = {}
+        square_sum = {}
         mean_var = {}
         rstd = {}
         y = {}
@@ -342,21 +342,34 @@ def tile_quantumsuperposition_t_kernel(
                 )
             sup[t] = sup_tile
 
-        def tile_statistics_on_scalar(t):
-            u, i = divmod(t, GROUP_TILES)
-            square = tail_pool.tile([P, Q], BF16, name="square")
-            row_sum = tail_pool.tile([P, 1], F32, name="row_sum")
-            nc.scalar.activation(out=square[:], in_=sup[t][:], func=ACT.Copy, accum_out=row_sum[:])
-            minus_mean_t = tail_pool.tile([P, 1], F32, name="minus_mean")
-            nc.scalar.activation(out=minus_mean_t[:], in_=row_sum[:], func=ACT.Copy, scale=-1.0 / Q)
-            minus_mean[t] = minus_mean_t
-            square_sum = tail_pool.tile([P, 1], F32, name="square_sum")
+        def scalar_sum(t):
+            ignored = tail_pool.tile([P, Q], BF16, name="ignored")
+            row_sum_t = tail_pool.tile([P, 1], F32, name="row_sum")
             nc.scalar.activation(
-                out=square[:], in_=sup[t][:], func=ACT.Square, bias=minus_mean_t[:, 0:1],
-                scale=1.0, accum_out=square_sum[:],
+                out=ignored[:], in_=sup[t][:], func=ACT.Copy, accum_out=row_sum_t[:]
             )
+            row_sum[t] = row_sum_t
+
+        def scalar_minus_mean(t):
+            minus_mean_t = tail_pool.tile([P, 1], F32, name="minus_mean")
             nc.scalar.activation(
-                out=mean_var[u][:, i, 1:2], in_=square_sum[:], func=ACT.Copy, scale=1.0 / Q
+                out=minus_mean_t[:], in_=row_sum[t][:], func=ACT.Copy, scale=-1.0 / Q
+            )
+            minus_mean[t] = minus_mean_t
+
+        def scalar_squares(t):
+            ignored = tail_pool.tile([P, Q], BF16, name="ignored")
+            square_sum_t = tail_pool.tile([P, 1], F32, name="square_sum")
+            nc.scalar.activation(
+                out=ignored[:], in_=sup[t][:], func=ACT.Square, bias=minus_mean[t][:, 0:1],
+                scale=1.0, accum_out=square_sum_t[:],
+            )
+            square_sum[t] = square_sum_t
+
+        def scalar_variance(t):
+            u, i = divmod(t, GROUP_TILES)
+            nc.scalar.activation(
+                out=mean_var[u][:, i, 1:2], in_=square_sum[t][:], func=ACT.Copy, scale=1.0 / Q
             )
 
         def tile_halves(t):
@@ -441,6 +454,8 @@ def tile_quantumsuperposition_t_kernel(
                 unit_rstd(u)
             if e == 3:
                 slice_mix(e)
+                nc.scalar.copy(out=gain[:], in_=spread_banks[0][:])
+                nc.scalar.copy(out=shift[:], in_=spread_banks[1][:])
                 for first in range(GROUP_TILES):
                     tile_transposes(first)
             if t == 0:
@@ -465,8 +480,10 @@ def tile_quantumsuperposition_t_kernel(
                 nc.scalar.activation(
                     out=warm_out[:], in_=eps[:], func=ACT.Abs_reciprocal_sqrt, bias=eps[:, 0:1], scale=1.0
                 )
+            if t in SCALAR_STATISTICS:
+                scalar_squares(t)
             if t + 1 in SCALAR_STATISTICS:
-                tile_statistics_on_scalar(t + 1)
+                scalar_sum(t + 1)
             elif 0 <= t + 1 < TILES:
                 tile_halves(t + 1)
             if t == -1:
@@ -493,7 +510,11 @@ def tile_quantumsuperposition_t_kernel(
                     tile_finish(last)
             elif t == TILES - 1:
                 unit_rstd(UNITS - 1, slice(2, 4))
-                for last in VECTOR_FINISHES:
+                for last in range(TILES - 2, TILES):
                     tile_finish(last)
             elif 0 <= t - LAG and t < TILES - 2:
                 tile_finish(t - LAG)
+            if t in SCALAR_STATISTICS:
+                scalar_variance(t)
+            if t + 1 in SCALAR_STATISTICS:
+                scalar_minus_mean(t + 1)

@@ -30,9 +30,9 @@ SLICES = UNITS * Q_SLICES
 SUP_BANKS = 4
 LEAD = GROUP_TILES + SUP_BANKS - 1
 ADD_TILES = 2
-SINGLE_ADDS = TILES - 8
+LAST_TILES = TILES - 12
 SCALAR_STATISTICS = (TILES - 6, TILES - 4, TILES - 2)
-VECTOR_FINISHES = (TILES - 2, TILES - 1)
+VECTOR_FINISHES = range(LAST_TILES + 1, TILES, 2)
 LAG = GROUP_TILES - 1
 
 TWO_PI_HIGH = 6.28125
@@ -107,9 +107,10 @@ def tile_quantumsuperposition_t_kernel(
         load_vec(nc.sync, amplitude_weights.rearrange("s (j p) -> (s j) p", p=P), per_vec, per_vec)
         load_x(0, slice(2, 4))
         load_w(0, pieces=2)
-        for s in range(1, STATES):
-            load_w(s)
-        for g in range(1, GROUPS):
+        load_w(1)
+        load_x(1)
+        load_w(2)
+        for g in range(2, GROUPS):
             load_x(g)
 
         ident = consts.tile([P, P], F32)
@@ -250,7 +251,9 @@ def tile_quantumsuperposition_t_kernel(
             spread(n, bank)
             spread_banks.append(bank)
         gain = consts.tile([P, Q], F32)
+        nc.scalar.copy(out=gain[:], in_=spread_banks[0][:])
         shift = consts.tile([P, Q], F32)
+        nc.scalar.copy(out=shift[:], in_=spread_banks[1][:])
 
         w_regroup(0, w_halves[0])
         total = consts.tile([P, Q_SLICES], F32)
@@ -270,50 +273,36 @@ def tile_quantumsuperposition_t_kernel(
         nc.vector.tensor_scalar(
             out=cosine[:], in0=sin_squared[:], scalar1=-2.0, scalar2=1.0, op0=ALU.mult, op1=ALU.add
         )
+        w_regroup(0, w_halves[1])
         mix = consts.tile(per_state, F32)
         nc.vector.tensor_mul(out=mix[:], in0=amplitudes[:], in1=cosine[:])
-        bias_mix = consts.tile(per_state, F32)
-        nc.vector.tensor_mul(out=bias_mix[:], in0=bias, in1=mix[:])
-        w_regroup(0, w_halves[1])
 
         acc = {}
         sup_t = {}
         sup = {}
         halves = {}
-        row_sum = {}
         minus_mean = {}
         square_sum = {}
         mean_var = {}
         rstd = {}
         y = {}
 
-        def slice_products(e):
+        def slice_products(e, times=1):
             u, j = divmod(e, Q_SLICES)
             g, s = divmod(u, STATES)
             cols = slice(s * Q + j * P, s * Q + (j + 1) * P)
             acc_e = psum_acc.tile([P, GROUP_ROWS], F32, name="acc")
-            nc.tensor.matmul_mx(
-                out=acc_e[:],
-                lhsT=w_codes[:, cols].bitcast(FP8X4),
-                lhsT_scale=w_scales[:, cols],
-                rhs=x_codes[g][:].bitcast(FP8X4),
-                rhs_scale=x_scales[g][:],
-                start=True,
-                stop=True,
-            )
+            for repeat in range(times):
+                nc.tensor.matmul_mx(
+                    out=acc_e[:],
+                    lhsT=w_codes[:, cols].bitcast(FP8X4),
+                    lhsT_scale=w_scales[:, cols],
+                    rhs=x_codes[g][:].bitcast(FP8X4),
+                    rhs_scale=x_scales[g][:],
+                    start=True,
+                    stop=True,
+                )
             acc[e] = acc_e
-
-        def keep_clock_up(g):
-            idle = psum_x.tile([P, Q], F32, name="small")
-            nc.tensor.matmul_mx(
-                out=idle[:],
-                lhsT=w_codes[:, 0:P].bitcast(FP8X4),
-                lhsT_scale=w_scales[:, 0:P],
-                rhs=x_codes[g][:].bitcast(FP8X4),
-                rhs_scale=x_scales[g][:],
-                start=True,
-                stop=True,
-            )
 
         def slice_mix(e):
             u, j = divmod(e, Q_SLICES)
@@ -321,17 +310,10 @@ def tile_quantumsuperposition_t_kernel(
             if j == 0:
                 sup_t_u = sup_t_pool.tile([P, Q_SLICES, GROUP_ROWS], F32, name="sup_t")
                 sup_t[u] = sup_t_u
-            if e == 1:
-                nc.vector.tensor_scalar(
-                    out=sup_t[u][:, j, :], in0=acc[e][:],
-                    scalar1=mix[:, s, j : j + 1], scalar2=bias_mix[:, s, j : j + 1],
-                    op0=ALU.mult, op1=ALU.add,
-                )
-            else:
-                nc.scalar.activation(
-                    out=sup_t[u][:, j, :], in_=acc[e][:], func=ACT.Identity,
-                    scale=mix[:, s, j : j + 1], bias=bias_mix[:, s, j : j + 1],
-                )
+            nc.scalar.activation(
+                out=sup_t[u][:, j, :], in_=acc[e][:], func=ACT.Identity,
+                scale=mix[:, s, j : j + 1], bias=bias_mix[:, s, j : j + 1],
+            )
 
         def tile_transposes(t):
             u, i = divmod(t, GROUP_TILES)
@@ -342,18 +324,12 @@ def tile_quantumsuperposition_t_kernel(
                 )
             sup[t] = sup_tile
 
-        def scalar_sum(t):
-            ignored = tail_pool.tile([P, Q], BF16, name="ignored")
-            row_sum_t = tail_pool.tile([P, 1], F32, name="row_sum")
-            nc.scalar.activation(
-                out=ignored[:], in_=sup[t][:], func=ACT.Copy, accum_out=row_sum_t[:]
-            )
-            row_sum[t] = row_sum_t
-
         def scalar_minus_mean(t):
+            ignored = tail_pool.tile([P, Q], BF16, name="ignored")
             minus_mean_t = tail_pool.tile([P, 1], F32, name="minus_mean")
             nc.scalar.activation(
-                out=minus_mean_t[:], in_=row_sum[t][:], func=ACT.Copy, scale=-1.0 / Q
+                out=ignored[:], in_=sup[t][:], func=ACT.Copy, scale=-1.0 / Q,
+                accum_out=minus_mean_t[:],
             )
             minus_mean[t] = minus_mean_t
 
@@ -428,9 +404,9 @@ def tile_quantumsuperposition_t_kernel(
                 nc.scalar.activation(
                     out=pair[:, n, :], in_=pair[:, n, :], func=ACT.Copy, scale=tile_rstd
                 )
-                if t < SINGLE_ADDS and n < ADD_TILES - 1:
+                if t < LAST_TILES and n < ADD_TILES - 1:
                     return
-                tiles = slice(n, n + 1) if t >= SINGLE_ADDS else slice(0, ADD_TILES)
+                tiles = slice(n, n + 1) if t >= LAST_TILES else slice(0, ADD_TILES)
                 per_add = tiles.stop - tiles.start
                 nc.gpsimd.tensor_tensor(
                     out=pair[:, tiles, :], in0=pair[:, tiles, :],
@@ -443,6 +419,8 @@ def tile_quantumsuperposition_t_kernel(
         slice_products(0)
         slice_products(1)
         w_quantise(0, w_halves[1])
+        bias_mix = consts.tile(per_state, F32)
+        nc.vector.tensor_mul(out=bias_mix[:], in0=bias, in1=mix[:])
         for t in range(-LEAD, TILES + LAG):
             u, i = divmod(t, GROUP_TILES)
             e = t + LEAD
@@ -450,28 +428,34 @@ def tile_quantumsuperposition_t_kernel(
             g = ahead // STATES
             if 0 <= t + 1 < TILES:
                 unit_statistics((t + 1) // GROUP_TILES)
-            if i == LAG and 0 <= u < UNITS - 1:
+            if i == LAG and 0 < u < UNITS - 1:
                 unit_rstd(u)
+            if t in (1, 3):
+                unit_rstd(0, slice(t - 1, t + 1))
             if e == 3:
                 slice_mix(e)
-                nc.scalar.copy(out=gain[:], in_=spread_banks[0][:])
-                nc.scalar.copy(out=shift[:], in_=spread_banks[1][:])
+                for pair in range(2):
+                    bank = psum_acc.tile([P, Q], F32, name="acc")
+                    x_transposes(1, pair, bank)
+                x_regroup(1, 0, nc.scalar.copy)
+                x_regroup(1, 1, nc.scalar.copy)
                 for first in range(GROUP_TILES):
                     tile_transposes(first)
-            if t == 0:
-                w_quantise(2)
+            if t == 1:
+                x_quantise(1)
             if e % 2 == 1 and e + 2 < SLICES:
-                slice_products(e + 1)
+                slice_products(e + 1, times=2)
                 slice_products(e + 2)
-                keep_clock_up(g)
-            if g + 1 < GROUPS:
+            if 0 < g and g + 1 < GROUPS:
                 if ahead % STATES == 1 and j % 2 == 1:
                     bank = psum_x.tile([P, Q], F32, name="small")
                     x_transposes(g + 1, j // 2, bank)
             if e < SLICES and e != 3:
                 slice_mix(e)
-            if g + 1 < GROUPS and ahead % STATES == 1 and j == 2:
+            if 0 < g and g + 1 < GROUPS and ahead % STATES == 1 and j == 2:
                 x_regroup(g + 1, 0, nc.scalar.copy)
+            if 0 < g and g + 1 < GROUPS and ahead % STATES == 2 and j == 0 and g > 0:
+                x_regroup(g + 1, 1, nc.scalar.copy)
             if e == 1:
                 w_regroup(1)
             if e == 2:
@@ -483,25 +467,27 @@ def tile_quantumsuperposition_t_kernel(
             if t in SCALAR_STATISTICS:
                 scalar_squares(t)
             if t + 1 in SCALAR_STATISTICS:
-                scalar_sum(t + 1)
+                scalar_minus_mean(t + 1)
             elif 0 <= t + 1 < TILES:
                 tile_halves(t + 1)
-            if t == -1:
+            if e == 3:
                 w_regroup(2)
-            if g + 1 < GROUPS and ahead % STATES == 2 and j == 1:
+            if t == -1:
+                w_quantise(2)
+            if 0 < g and g + 1 < GROUPS and ahead % STATES == 2 and j == 1 and not (g > 0):
                 x_regroup(g + 1, 1, nc.vector.tensor_copy)
-            if g + 1 < GROUPS and ahead % STATES == 2 and j == 2:
-                x_quantise(g + 1)
             if 0 <= t < TILES:
                 tile_centre_and_gain(t)
+            if 0 < g and g + 1 < GROUPS and ahead % STATES == 2 and j == 2:
+                x_quantise(g + 1)
             if 0 <= t + 1 < TILES and t + 1 not in SCALAR_STATISTICS:
                 tile_mean_var(t + 1)
             if t % 2 == 0:
                 for ahead_t in (t + SUP_BANKS - 1, t + SUP_BANKS):
                     if GROUP_TILES <= ahead_t < TILES:
                         tile_transposes(ahead_t)
-            if t == TILES - LEAD + 2:
-                bank = psum_acc.tile([P, Q], F32, name="acc")
+            if t == LAST_TILES + 2:
+                bank = psum_x.tile([P, Q], F32, name="small")
                 spread(1, bank)
                 shift_bank.append(bank)
             if t == TILES - 2:
@@ -512,9 +498,9 @@ def tile_quantumsuperposition_t_kernel(
                 unit_rstd(UNITS - 1, slice(2, 4))
                 for last in range(TILES - 2, TILES):
                     tile_finish(last)
-            elif 0 <= t - LAG and t < TILES - 2:
+            elif 0 <= t - 1 < GROUP_TILES:
+                tile_finish(t - 1)
+            elif GROUP_TILES <= t - LAG and t < TILES - 2:
                 tile_finish(t - LAG)
             if t in SCALAR_STATISTICS:
                 scalar_variance(t)
-            if t + 1 in SCALAR_STATISTICS:
-                scalar_minus_mean(t + 1)

from contextlib import ExitStack

import concourse.mybir as mybir
from concourse.masks import make_identity

F32 = mybir.dt.float32
BF16 = mybir.dt.bfloat16
U32 = mybir.dt.uint32
U8 = mybir.dt.uint8
FP8X4 = mybir.dt.float8_e4m3fn_x4
ALU = mybir.AluOpType
ACT = mybir.ActivationFunctionType

P = 128
ROWS = 4096
K = 512
Q = 512
STATES = 3
LN_EPS = 1e-5

PACK = 4
ROW_TILES = ROWS // P
GROUP_TILES = 4
GROUP_ROWS = GROUP_TILES * P
GROUPS = ROW_TILES // GROUP_TILES
Q_SLICES = Q // P
UNITS = GROUPS * STATES
TILES = UNITS * GROUP_TILES
SLICES = UNITS * Q_SLICES
SUP_BANKS = 4
LEAD = GROUP_TILES + SUP_BANKS - 1
ADD_TILES = 2
LAST_TILES = TILES - 12
SCALAR_STATISTICS = (TILES - 6, TILES - 4, TILES - 2)
VECTOR_FINISHES = range(LAST_TILES + 1, TILES, 2)
LAG = GROUP_TILES - 1

TWO_PI_HIGH = 6.28125
TWO_PI_MID = 0.0019350051879882812
TWO_PI_LOW = 3.019916050561733e-07
ONE_OVER_TWO_PI = 0.15915494309189535
ROUND_TO_WHOLE = 12582912.0

FLOPS = 2 * ROWS * STATES * K * Q


def tile_quantumsuperposition_t_kernel(
    tc, language_features, W, b, amplitude_weights, phase_weights, ln_gamma, ln_beta, out
):
    nc = tc.nc
    with ExitStack() as ctx:
        consts = ctx.enter_context(tc.tile_pool(name="consts", bufs=1))
        x_in = ctx.enter_context(tc.tile_pool(name="x_in", bufs=GROUPS))
        x_mx = ctx.enter_context(tc.tile_pool(name="x_mx", bufs=2))
        w_in = ctx.enter_context(tc.tile_pool(name="w_in", bufs=STATES))
        sup_t_pool = ctx.enter_context(tc.tile_pool(name="sup_t", bufs=3))
        tail_pool = ctx.enter_context(tc.tile_pool(name="tail", bufs=2))
        y_pool = ctx.enter_context(tc.tile_pool(name="y", bufs=8))
        stat_pool = ctx.enter_context(tc.tile_pool(name="stat", bufs=4))
        psum_acc = ctx.enter_context(tc.psum_pool(name="psum_acc", bufs=3))
        psum_sup = ctx.enter_context(tc.psum_pool(name="psum_sup", bufs=SUP_BANKS))
        psum_x = ctx.enter_context(tc.psum_pool(name="psum_x", bufs=1))
        ctx.enter_context(tc.manual_schedule())

        x_view = language_features.rearrange("(p i) k -> p i k", i=ROW_TILES)
        out_view = out.rearrange("(p i) s q -> p i s q", i=ROW_TILES)

        vec_rows = consts.tile([P, P], BF16)
        nc.vector.memset(vec_rows[:], 0.0)
        per_vec = STATES * Q_SLICES
        vec_columns = 3 * per_vec + 2 * Q_SLICES

        def load_vec(queue, vec, first_row, rows):
            queue.dma_start(out=vec_rows[first_row : first_row + rows, :], in_=vec)

        load_vec(nc.scalar, b.rearrange("s (j p) -> (s j) p", p=P), 2 * per_vec, per_vec)
        load_vec(nc.scalar, ln_gamma.rearrange("(j p) -> j p", p=P), 3 * per_vec, Q_SLICES)
        load_vec(
            nc.scalar, ln_beta.rearrange("(j p) -> j p", p=P), 3 * per_vec + Q_SLICES, Q_SLICES
        )

        w_rows = {}
        x_rows = {}

        def load_w(s, pieces=1):
            rows = w_in.tile([P, PACK * Q], BF16, name="w_rows")
            rows_view = rows[:].rearrange("p (t q) -> p t q", t=PACK)
            w_view = W[s, :, :].rearrange("(p t) q -> p t q", t=PACK)
            for n in range(pieces):
                cols = slice(n * Q // pieces, (n + 1) * Q // pieces)
                nc.sync.dma_start(out=rows_view[:, :, cols], in_=w_view[:, :, cols])
            w_rows[s] = rows

        def load_x(g, tiles=slice(0, GROUP_TILES)):
            if g not in x_rows:
                rows = x_in.tile([P, GROUP_TILES * K], BF16, name="x_rows")
                x_rows[g] = rows
            rows_view = x_rows[g][:].rearrange("p (i k) -> p i k", i=GROUP_TILES)
            first = g * GROUP_TILES
            nc.sync.dma_start(
                out=rows_view[:, tiles, :],
                in_=x_view[:, first + tiles.start : first + tiles.stop, :],
            )

        load_x(0, slice(0, 2))
        load_vec(nc.sync, phase_weights.rearrange("s (j p) -> (s j) p", p=P), 0, per_vec)
        load_vec(nc.sync, amplitude_weights.rearrange("s (j p) -> (s j) p", p=P), per_vec, per_vec)
        load_x(0, slice(2, 4))
        load_w(0, pieces=2)
        load_w(1)
        load_x(1)
        load_w(2)
        for g in range(2, GROUPS):
            load_x(g)

        ident = consts.tile([P, P], F32)
        make_identity(nc, ident[:])
        eps = consts.tile([P, 1], F32)
        nc.vector.memset(eps[:], LN_EPS)
        warm_in = consts.tile([P, 1], F32)
        nc.vector.memset(warm_in[:], 0.0)
        warm_out = consts.tile([P, 1], F32)
        nc.scalar.activation(out=warm_out[:], in_=warm_in[:], func=ACT.Exp)

        w_codes = consts.tile([P, STATES * Q], U32, align_bytes=64)
        w_scales = consts.tile([P, STATES * Q], U8, align_bytes=64)
        w_grouped = {}

        def w_regroup(s, cols=slice(0, Q)):
            grouped = w_in.tile([P, (cols.stop - cols.start) * PACK], BF16, name="w_grouped", align_bytes=64)
            nc.vector.tensor_copy(
                out=grouped[:].rearrange("p (q t) -> p q t", t=PACK),
                in_=w_rows[s][:].rearrange("p (t q) -> p q t", t=PACK)[:, cols, :],
            )
            w_grouped[s, cols.start] = grouped

        def w_quantise(s, cols=slice(0, Q)):
            codes = slice(s * Q + cols.start, s * Q + cols.stop)
            nc.vector.quantize_mx(
                out=w_codes[:, codes].bitcast(FP8X4),
                scales=w_scales[:, codes],
                in_=w_grouped[s, cols.start][:],
            )

        w_halves = (slice(0, Q // 2), slice(Q // 2, Q))

        x_t = {}
        x_grouped = {}
        x_codes = {}
        x_scales = {}

        def x_transposes(g, pair, bank):
            words = x_rows[g][:].bitcast(F32)
            for ii in range(2):
                for u in range(2):
                    first = (2 * pair + ii) * 2 * P
                    column = (2 * u + ii) * P
                    nc.tensor.transpose(
                        bank[:, column : column + P],
                        words[:, first + u : first + 2 * P : 2],
                        ident[:],
                    )
            x_t[g, pair] = bank

        def x_regroup(g, pair, copy):
            if g not in x_grouped:
                grouped = x_mx.tile([P, GROUP_ROWS * PACK], BF16, name="x_grouped", align_bytes=64)
                x_grouped[g] = grouped
            grouped_words = x_grouped[g][:].bitcast(F32).rearrange("p (c u) -> p c u", u=2)
            copy(
                out=grouped_words[:, pair * 2 * P : (pair + 1) * 2 * P, :],
                in_=x_t[g, pair][:].rearrange("p (u c) -> p c u", u=2),
            )

        def x_quantise(g):
            codes = x_mx.tile([P, GROUP_ROWS], U32, name="x_codes", align_bytes=64)
            scales = x_mx.tile([P, GROUP_ROWS], U8, name="x_scales", align_bytes=64)
            nc.vector.quantize_mx(
                out=codes[:].bitcast(FP8X4), scales=scales[:], in_=x_grouped[g][:]
            )
            x_codes[g] = codes
            x_scales[g] = scales

        def first_rows(pair, copy):
            bank = psum_acc.tile([P, Q], F32, name="acc")
            x_transposes(0, pair, bank)
            x_regroup(0, pair, copy)

        first_rows(0, nc.scalar.copy)
        vec_rows_f32 = consts.tile([P, P], F32)
        nc.vector.tensor_copy(out=vec_rows_f32[:], in_=vec_rows[:])
        vec_t = psum_x.tile([P, Q], F32, name="small")
        nc.tensor.transpose(vec_t[:, 0:P], vec_rows_f32[:], ident[:])
        vecs = consts.tile([P, vec_columns], F32)
        nc.vector.tensor_copy(out=vecs[:], in_=vec_t[:, 0:vec_columns])

        def per_state_columns(n):
            return vecs[:, n * per_vec : (n + 1) * per_vec].rearrange("p (s j) -> p s j", s=STATES)

        phase = per_state_columns(0)
        amplitude = per_state_columns(1)
        bias = per_state_columns(2)
        per_state = [P, STATES, Q_SLICES]

        def spread(n, bank):
            for j in range(Q_SLICES):
                column = 3 * per_vec + n * Q_SLICES + j
                nc.tensor.transpose(
                    bank[:, j * P : (j + 1) * P],
                    vecs[:, column : column + 1].to_broadcast([P, P]),
                    ident[:],
                )

        shift_bank = []

        turns = consts.tile(per_state, F32)
        nc.gpsimd.tensor_scalar(
            out=turns[:], in0=phase, scalar1=ONE_OVER_TWO_PI, scalar2=ROUND_TO_WHOLE,
            op0=ALU.mult, op1=ALU.add,
        )
        nc.gpsimd.tensor_scalar(
            out=turns[:], in0=turns[:], scalar1=ROUND_TO_WHOLE, scalar2=0.0,
            op0=ALU.subtract, op1=ALU.add,
        )
        rest = consts.tile(per_state, F32)
        nc.gpsimd.tensor_copy(out=rest[:], in_=phase)
        for part in (TWO_PI_HIGH, TWO_PI_MID, TWO_PI_LOW):
            taken = consts.tile(per_state, F32, name="taken")
            nc.gpsimd.tensor_scalar(
                out=taken[:], in0=turns[:], scalar1=part, scalar2=0.0, op0=ALU.mult, op1=ALU.add
            )
            nc.gpsimd.tensor_tensor(out=rest[:], in0=rest[:], in1=taken[:], op=ALU.subtract)

        top = consts.tile([P, Q_SLICES], F32)
        nc.vector.tensor_max(out=top[:], in0=amplitude[:, 0, :], in1=amplitude[:, 1, :])
        nc.vector.tensor_max(out=top[:], in0=top[:], in1=amplitude[:, 2, :])
        shifted = consts.tile(per_state, F32)
        nc.vector.tensor_tensor(
            out=shifted[:], in0=amplitude, in1=top[:].unsqueeze(1).to_broadcast(per_state),
            op=ALU.subtract,
        )
        expd = consts.tile(per_state, F32)
        nc.scalar.activation(out=expd[:], in_=shifted[:], func=ACT.Exp)
        half_sin = consts.tile(per_state, F32)
        nc.scalar.activation(out=half_sin[:], in_=rest[:], func=ACT.Sin, scale=0.5)

        first_rows(1, nc.vector.tensor_copy)
        spread_banks = []
        for n in range(2):
            bank = psum_sup.tile([P, Q], F32, name="sup")
            spread(n, bank)
            spread_banks.append(bank)
        gain = consts.tile([P, Q], F32)
        nc.scalar.copy(out=gain[:], in_=spread_banks[0][:])
        shift = consts.tile([P, Q], F32)
        nc.scalar.copy(out=shift[:], in_=spread_banks[1][:])

        w_regroup(0, w_halves[0])
        total = consts.tile([P, Q_SLICES], F32)
        nc.vector.tensor_add(out=total[:], in0=expd[:, 0, :], in1=expd[:, 1, :])
        x_quantise(0)
        nc.vector.tensor_add(out=total[:], in0=total[:], in1=expd[:, 2, :])
        w_quantise(0, w_halves[0])
        one_over_total = consts.tile([P, Q_SLICES], F32)
        nc.vector.reciprocal(out=one_over_total[:], in_=total[:])
        sin_squared = consts.tile(per_state, F32)
        nc.vector.tensor_mul(out=sin_squared[:], in0=half_sin[:], in1=half_sin[:])
        amplitudes = consts.tile(per_state, F32)
        nc.vector.tensor_mul(
            out=amplitudes[:], in0=expd[:], in1=one_over_total[:].unsqueeze(1).to_broadcast(per_state)
        )
        cosine = consts.tile(per_state, F32)
        nc.vector.tensor_scalar(
            out=cosine[:], in0=sin_squared[:], scalar1=-2.0, scalar2=1.0, op0=ALU.mult, op1=ALU.add
        )
        w_regroup(0, w_halves[1])
        mix = consts.tile(per_state, F32)
        nc.vector.tensor_mul(out=mix[:], in0=amplitudes[:], in1=cosine[:])

        acc = {}
        sup_t = {}
        sup = {}
        halves = {}
        minus_mean = {}
        square_sum = {}
        mean_var = {}
        rstd = {}
        y = {}

        def slice_products(e, times=1):
            u, j = divmod(e, Q_SLICES)
            g, s = divmod(u, STATES)
            cols = slice(s * Q + j * P, s * Q + (j + 1) * P)
            acc_e = psum_acc.tile([P, GROUP_ROWS], F32, name="acc")
            for repeat in range(times):
                nc.tensor.matmul_mx(
                    out=acc_e[:],
                    lhsT=w_codes[:, cols].bitcast(FP8X4),
                    lhsT_scale=w_scales[:, cols],
                    rhs=x_codes[g][:].bitcast(FP8X4),
                    rhs_scale=x_scales[g][:],
                    start=True,
                    stop=True,
                )
            acc[e] = acc_e

        def slice_mix(e):
            u, j = divmod(e, Q_SLICES)
            s = u % STATES
            if j == 0:
                sup_t_u = sup_t_pool.tile([P, Q_SLICES, GROUP_ROWS], F32, name="sup_t")
                sup_t[u] = sup_t_u
            nc.scalar.activation(
                out=sup_t[u][:, j, :], in_=acc[e][:], func=ACT.Identity,
                scale=mix[:, s, j : j + 1], bias=bias_mix[:, s, j : j + 1],
            )

        def tile_transposes(t):
            u, i = divmod(t, GROUP_TILES)
            sup_tile = psum_sup.tile([P, Q], F32, name="sup")
            for j in range(Q_SLICES):
                nc.tensor.transpose(
                    sup_tile[:, j * P : (j + 1) * P], sup_t[u][:, j, i * P : (i + 1) * P], ident[:]
                )
            sup[t] = sup_tile

        def scalar_minus_mean(t):
            ignored = tail_pool.tile([P, Q], BF16, name="ignored")
            minus_mean_t = tail_pool.tile([P, 1], F32, name="minus_mean")
            nc.scalar.activation(
                out=ignored[:], in_=sup[t][:], func=ACT.Copy, scale=-1.0 / Q,
                accum_out=minus_mean_t[:],
            )
            minus_mean[t] = minus_mean_t

        def scalar_squares(t):
            ignored = tail_pool.tile([P, Q], BF16, name="ignored")
            square_sum_t = tail_pool.tile([P, 1], F32, name="square_sum")
            nc.scalar.activation(
                out=ignored[:], in_=sup[t][:], func=ACT.Square, bias=minus_mean[t][:, 0:1],
                scale=1.0, accum_out=square_sum_t[:],
            )
            square_sum[t] = square_sum_t

        def scalar_variance(t):
            u, i = divmod(t, GROUP_TILES)
            nc.scalar.activation(
                out=mean_var[u][:, i, 1:2], in_=square_sum[t][:], func=ACT.Copy, scale=1.0 / Q
            )

        def tile_halves(t):
            halves_t = stat_pool.tile([P, 6], F32, name="halves")
            nc.vector.bn_stats(out=halves_t[:], in_=sup[t][:])
            halves[t] = halves_t

        def unit_statistics(u):
            if u not in mean_var:
                mean_var_u = stat_pool.tile([P, GROUP_TILES, 2], F32, name="mean_var")
                mean_var[u] = mean_var_u

        def tile_mean_var(t):
            u, i = divmod(t, GROUP_TILES)
            nc.vector.bn_aggr(out=mean_var[u][:, i, :], in_=halves[t][:])

        def tile_centre_and_gain(t):
            u, i = divmod(t, GROUP_TILES)
            if t % ADD_TILES == 0:
                y_pair = y_pool.tile([P, ADD_TILES, Q], F32, name="y")
                y[t // ADD_TILES] = y_pair
            y_t = y[t // ADD_TILES][:, t % ADD_TILES, :]
            if t in SCALAR_STATISTICS:
                nc.vector.scalar_tensor_tensor(
                    out=y_t, in0=sup[t][:], scalar=minus_mean[t][:, 0:1], in1=gain[:],
                    op0=ALU.add, op1=ALU.mult,
                )
            else:
                nc.vector.scalar_tensor_tensor(
                    out=y_t, in0=sup[t][:], scalar=mean_var[u][:, i, 0:1], in1=gain[:],
                    op0=ALU.subtract, op1=ALU.mult,
                )

        def unit_rstd(u, tiles=slice(0, GROUP_TILES)):
            if u not in rstd:
                rstd_u = stat_pool.tile([P, GROUP_TILES], F32, name="rstd")
                rstd[u] = rstd_u
            nc.scalar.activation(
                out=rstd[u][:, tiles], in_=mean_var[u][:, tiles, 1], func=ACT.Abs_reciprocal_sqrt,
                bias=eps[:, 0:1], scale=1.0,
            )

        def tile_finish(t):
            u, i = divmod(t, GROUP_TILES)
            g, s = divmod(u, STATES)
            pair = y[t // ADD_TILES]
            n = t % ADD_TILES
            tile_rstd = rstd[u][:, i : i + 1]
            if t in VECTOR_FINISHES:
                nc.vector.scalar_tensor_tensor(
                    out=pair[:, n, :], in0=pair[:, n, :], scalar=tile_rstd, in1=shift_bank[0][:],
                    op0=ALU.mult, op1=ALU.add,
                )
                tiles = slice(n, n + 1)
            else:
                nc.scalar.activation(
                    out=pair[:, n, :], in_=pair[:, n, :], func=ACT.Copy, scale=tile_rstd
                )
                if t < LAST_TILES and n < ADD_TILES - 1:
                    return
                tiles = slice(n, n + 1) if t >= LAST_TILES else slice(0, ADD_TILES)
                per_add = tiles.stop - tiles.start
                nc.gpsimd.tensor_tensor(
                    out=pair[:, tiles, :], in0=pair[:, tiles, :],
                    in1=shift[:].unsqueeze(1).to_broadcast([P, per_add, Q]), op=ALU.add,
                )
            first = g * GROUP_TILES + i + tiles.start - n
            last = g * GROUP_TILES + i + tiles.stop - n
            nc.sync.dma_start(out=out_view[:, first:last, s, :], in_=pair[:, tiles, :])

        slice_products(0)
        slice_products(1)
        w_quantise(0, w_halves[1])
        bias_mix = consts.tile(per_state, F32)
        nc.vector.tensor_mul(out=bias_mix[:], in0=bias, in1=mix[:])
        for t in range(-LEAD, TILES + LAG):
            u, i = divmod(t, GROUP_TILES)
            e = t + LEAD
            ahead, j = divmod(e, Q_SLICES)
            g = ahead // STATES
            if 0 <= t + 1 < TILES:
                unit_statistics((t + 1) // GROUP_TILES)
            if i == LAG and 0 < u < UNITS - 1:
                unit_rstd(u)
            if t in (1, 3):
                unit_rstd(0, slice(t - 1, t + 1))
            if e == 3:
                slice_mix(e)
                for pair in range(2):
                    bank = psum_acc.tile([P, Q], F32, name="acc")
                    x_transposes(1, pair, bank)
                x_regroup(1, 0, nc.scalar.copy)
                x_regroup(1, 1, nc.scalar.copy)
                for first in range(GROUP_TILES):
                    tile_transposes(first)
            if t == 1:
                x_quantise(1)
            if e % 2 == 1 and e + 2 < SLICES:
                slice_products(e + 1, times=2)
                slice_products(e + 2)
            if 0 < g and g + 1 < GROUPS:
                if ahead % STATES == 1 and j % 2 == 1:
                    bank = psum_x.tile([P, Q], F32, name="small")
                    x_transposes(g + 1, j // 2, bank)
            if e < SLICES and e != 3:
                slice_mix(e)
            if 0 < g and g + 1 < GROUPS and ahead % STATES == 1 and j == 2:
                x_regroup(g + 1, 0, nc.scalar.copy)
            if 0 < g and g + 1 < GROUPS and ahead % STATES == 2 and j == 0 and g > 0:
                x_regroup(g + 1, 1, nc.scalar.copy)
            if e == 1:
                w_regroup(1)
            if e == 2:
                w_quantise(1)
            if e == 3:
                nc.scalar.activation(
                    out=warm_out[:], in_=eps[:], func=ACT.Abs_reciprocal_sqrt, bias=eps[:, 0:1], scale=1.0
                )
            if t in SCALAR_STATISTICS:
                scalar_squares(t)
            if t + 1 in SCALAR_STATISTICS:
                scalar_minus_mean(t + 1)
            elif 0 <= t + 1 < TILES:
                tile_halves(t + 1)
            if e == 3:
                w_regroup(2)
            if t == -1:
                w_quantise(2)
            if 0 < g and g + 1 < GROUPS and ahead % STATES == 2 and j == 1 and not (g > 0):
                x_regroup(g + 1, 1, nc.vector.tensor_copy)
            if 0 <= t < TILES:
                tile_centre_and_gain(t)
            if 0 < g and g + 1 < GROUPS and ahead % STATES == 2 and j == 2:
                x_quantise(g + 1)
            if 0 <= t + 1 < TILES and t + 1 not in SCALAR_STATISTICS:
                tile_mean_var(t + 1)
            if t % 2 == 0:
                for ahead_t in (t + SUP_BANKS - 1, t + SUP_BANKS):
                    if GROUP_TILES <= ahead_t < TILES:
                        tile_transposes(ahead_t)
            if t == LAST_TILES + 2:
                bank = psum_x.tile([P, Q], F32, name="small")
                spread(1, bank)
                shift_bank.append(bank)
            if t == TILES - 2:
                unit_rstd(UNITS - 1, slice(0, 2))
                for last in range(TILES - 5, TILES - 2):
                    tile_finish(last)
            elif t == TILES - 1:
                unit_rstd(UNITS - 1, slice(2, 4))
                for last in range(TILES - 2, TILES):
                    tile_finish(last)
            elif 0 <= t - 1 < GROUP_TILES:
                tile_finish(t - 1)
            elif GROUP_TILES <= t - LAG and t < TILES - 2:
                tile_finish(t - LAG)
            if t in SCALAR_STATISTICS:
                scalar_variance(t)
